import numpy as np
import ml_dtypes


def mxq(x, axis, fmt="e4m3"):
    dtype, down = {"e4m3": (ml_dtypes.float8_e4m3fn, 7), "e5m2": (ml_dtypes.float8_e5m2, 14)}[fmt]
    v = np.moveaxis(np.asarray(x, np.float32).astype(ml_dtypes.bfloat16).astype(np.float64), axis, -1)
    blocks = v.reshape(v.shape[:-1] + (-1, 32))
    amax = np.abs(blocks).max(-1, keepdims=True)
    byte = np.maximum(np.where(amax > 0, np.frexp(amax)[1] - 1 + 127, 0) - down, 1)
    scale = np.exp2(byte - 127.0)
    codes = (blocks / scale).astype(np.float32).astype(dtype).astype(np.float64)
    return np.moveaxis((codes * scale).reshape(v.shape), -1, axis)


WIDE = False


def mx_kscale(k):
    if not WIDE:
        return np.ones(k)
    levels = np.array([10, -10, 5, -5, 0])
    if k % 512:
        return np.exp2(np.random.permutation(np.resize(levels, k // 32))).repeat(32)
    a = np.empty((k // 512, 16))
    for p in range(k // 512):
        a[p, :8] = np.random.permutation(np.resize(levels, 8))
        for g in range(8):
            far = levels[np.abs(levels - a[p, g]) >= 10]
            a[p, g + 8] = far[np.random.randint(len(far))]
    return np.exp2(a.ravel()).repeat(32)


BF16 = ml_dtypes.bfloat16


def bf(x):
    return np.asarray(x, np.float32).astype(BF16)


def f64(x):
    return np.asarray(x).astype(np.float64)


N, K, D_IN, HC, H = 256, 8, 1024, 1024, 1024


def sigmoid(v):
    return 1.0 / (1.0 + np.exp(-v))


def setup_inputs():
    s, t = mx_kscale(D_IN), mx_kscale(HC)
    d = {
        "x": bf(np.random.standard_normal((N, D_IN)) * s),
        "child_h": bf(np.random.standard_normal((N, K, HC)) * t),
        "fc_sum": bf(np.random.standard_normal((N, H)) * 0.27 * np.sqrt(K)),
    }
    for g in ("i", "o", "u"):
        d["W" + g] = bf(np.random.standard_normal((D_IN, H)) * 0.7 / np.sqrt(D_IN) / s[:, None])
        d["bW" + g] = bf(np.random.standard_normal(H) * 0.3)
        d["U" + g] = bf(np.random.standard_normal((HC, H)) * 0.7 / np.sqrt(K * HC) / t[:, None])
        d["bU" + g] = bf(np.random.standard_normal(H) * 0.3)
    return d


def reference(x, child_h, fc_sum, Wi, bWi, Ui, bUi, Wo, bWo, Uo, bUo, Wu, bWu, Uu, bUu):
    h_sum = f64(child_h).sum(axis=1)
    xq = mxq(f64(x), 1, "e4m3")
    hq = mxq(h_sum, 1, "e4m3")
    i = sigmoid((xq @ mxq(f64(Wi), 0, "e4m3")) + f64(bWi) + (hq @ mxq(f64(Ui), 0, "e4m3")) + f64(bUi))
    o = sigmoid((xq @ mxq(f64(Wo), 0, "e4m3")) + f64(bWo) + (hq @ mxq(f64(Uo), 0, "e4m3")) + f64(bUo))
    u = np.tanh((xq @ mxq(f64(Wu), 0, "e4m3")) + f64(bWu) + (hq @ mxq(f64(Uu), 0, "e4m3")) + f64(bUu))
    c = i * u + f64(fc_sum)
    h = o * np.tanh(c)
    return np.stack([h, c], axis=0)

@@ -1,0 +1,248 @@
+from contextlib import ExitStack
+
+import concourse.mybir as mybir
+from concourse.masks import make_identity
+
+F32 = mybir.dt.float32
+BF16 = mybir.dt.bfloat16
+U32 = mybir.dt.uint32
+U8 = mybir.dt.uint8
+FP8X4 = mybir.dt.float8_e4m3fn_x4
+ACT = mybir.ActivationFunctionType
+ALU = mybir.AluOpType
+
+P = 128
+PACK = 4
+K_PASS = P * PACK
+NODES = 256
+NODE_TILES = NODES // P
+CHILDREN = 8
+FEATURES = 1024
+PASSES = FEATURES // K_PASS
+HIDDEN = 1024
+COL_TILES = HIDDEN // P
+BANK = 512
+
+ROWS_PER_PARTITION = 4
+NODES_PER_LOAD = P * ROWS_PER_PARTITION // CHILDREN
+PARTITIONS_PER_NODE = P // NODES_PER_LOAD
+CHILD_LOADS = NODES // NODES_PER_LOAD
+
+GATE_I, GATE_U, GATE_O = 0, 1, 2
+
+VECTOR_COLS = 512
+
+FLOPS = 2 * NODES * FEATURES * HIDDEN * 6
+
+
+def tile_childsumtreelstmcell_pb_kernel(
+    tc, x, child_h, fc_sum, Wi, bWi, Ui, bUi, Wo, bWo, Uo, bUo, Wu, bWu, Uu, bUu, out
+):
+    nc = tc.nc
+    with ExitStack() as ctx:
+        const = ctx.enter_context(tc.tile_pool(name="const", bufs=1))
+        keep = ctx.enter_context(tc.tile_pool(name="keep", bufs=1))
+        raw_pool = ctx.enter_context(tc.tile_pool(name="raw", bufs=5))
+        grouped_pool = ctx.enter_context(tc.tile_pool(name="grouped", bufs=3))
+        child_pool = ctx.enter_context(tc.tile_pool(name="child", bufs=4))
+        psum = ctx.enter_context(tc.psum_pool(name="psum", bufs=8))
+
+        ident = const.tile([P, P], F32)
+        make_identity(nc, ident[:])
+        node_of_f32 = const.tile([P, NODES_PER_LOAD], F32)
+        nc.vector.reduce_sum(
+            out=node_of_f32[:],
+            in_=ident[:].rearrange("q (i r) -> q i r", r=PARTITIONS_PER_NODE),
+            axis=mybir.AxisListType.X,
+        )
+        node_of = const.tile([P, NODES_PER_LOAD], BF16)
+        nc.vector.tensor_copy(out=node_of[:], in_=node_of_f32[:])
+
+        zero_col = const.tile([P, 1], F32)
+        nc.vector.memset(zero_col[:], 0.0)
+        half_col = const.tile([P, 1], F32)
+        nc.scalar.activation(out=half_col[:], in_=zero_col[:], func=ACT.Sigmoid)
+
+        gate_biases = ((bWi, bUi), (bWu, bUu), (bWo, bUo))
+        bias_rows = const.tile([P, P], BF16)
+        nc.vector.memset(bias_rows[:], 0.0)
+        rows_per_gate = PARTITIONS_PER_NODE * COL_TILES
+        for m, pair_of_biases in enumerate(gate_biases):
+            for r, b in enumerate(pair_of_biases):
+                nc.scalar.dma_start(
+                    out=bias_rows[rows_per_gate * m + r : rows_per_gate * (m + 1) : PARTITIONS_PER_NODE, :],
+                    in_=b.rearrange("(j p) -> j p", p=P),
+                )
+        bias_ps = psum.tile([P, NODES_PER_LOAD], F32, tag="bank")
+        nc.tensor.matmul(out=bias_ps[:], lhsT=bias_rows[:], rhs=node_of[:], start=True, stop=True)
+        bias = const.tile([P, NODES_PER_LOAD], F32)
+        nc.vector.tensor_copy(out=bias[:], in_=bias_ps[:])
+
+        def quantise_weight(w, label):
+            quantised = []
+            for g in range(PASSES):
+                raw = raw_pool.tile([P, PACK, HIDDEN], BF16)
+                nc.sync.dma_start(
+                    out=raw[:],
+                    in_=w[K_PASS * g : K_PASS * (g + 1), :].rearrange("(p t) n -> p t n", t=PACK),
+                )
+                grouped = grouped_pool.tile([P, HIDDEN, PACK], BF16, align_bytes=64)
+                for copy, cols in (
+                    (nc.vector.tensor_copy, slice(0, VECTOR_COLS)),
+                    (nc.scalar.copy, slice(VECTOR_COLS, HIDDEN)),
+                ):
+                    copy(
+                        out=grouped[:, cols, :].rearrange("p (c i) t -> p c t i", i=4),
+                        in_=raw[:, :, cols].rearrange("p t (c i) -> p c t i", i=4),
+                    )
+                words = keep.tile([P, HIDDEN], U32, align_bytes=64, name="words_%s%d" % (label, g))
+                scales = keep.tile([P, HIDDEN], U8, align_bytes=64, name="scales_%s%d" % (label, g))
+                for cols in (slice(0, HIDDEN // 2), slice(HIDDEN // 2, HIDDEN)):
+                    nc.vector.quantize_mx(
+                        out=words[:, cols].bitcast(FP8X4),
+                        scales=scales[:, cols],
+                        in_=grouped[:, cols, :].rearrange("p n t -> p (n t)"),
+                    )
+                quantised.append((words, scales))
+            return quantised
+
+        def quantise_nodes(grouped, label):
+            words = keep.tile([P, PASSES, NODES], U32, align_bytes=64, name="words_" + label)
+            scales = keep.tile([P, PASSES, NODES], U8, align_bytes=64, name="scales_" + label)
+            nc.vector.quantize_mx(
+                out=words[:].rearrange("p g n -> p (g n)").bitcast(FP8X4),
+                scales=scales[:].rearrange("p g n -> p (g n)"),
+                in_=grouped[:].rearrange("p g n t -> p (g n t)"),
+            )
+            return words, scales
+
+        def gate(m, w_q, u_q, func, label):
+            result = keep.tile([P, COL_TILES, NODES], F32, name="gate_" + label)
+            acc = [psum.tile([P, NODES], F32, tag="bank", name="acc%d" % j) for j in range(COL_TILES)]
+
+            def mx_pass(j, weight_q, nodes_q, g, start, stop):
+                (w_words, w_scales), (a_words, a_scales) = weight_q[g], nodes_q
+                cols = slice(P * j, P * (j + 1))
+                nc.tensor.matmul_mx(
+                    out=acc[j][:],
+                    lhsT=w_words[:, cols].bitcast(FP8X4),
+                    lhsT_scale=w_scales[:, cols],
+                    rhs=a_words[:, g, :].bitcast(FP8X4),
+                    rhs_scale=a_scales[:, g, :],
+                    start=start,
+                    stop=stop,
+                )
+
+            for g in range(PASSES):
+                for j in range(COL_TILES):
+                    mx_pass(j, w_q, x_q, g, g == 0, False)
+            for j in range(COL_TILES):
+                for g in range(PASSES):
+                    mx_pass(j, u_q, h_q, g, False, g == PASSES - 1)
+                nc.scalar.activation(
+                    out=result[:, j, :],
+                    in_=acc[j][:],
+                    func=func,
+                    bias=bias[:, COL_TILES * m + j : COL_TILES * m + j + 1],
+                )
+            return result
+
+        def flip_back(source, half):
+            flipped = [psum.tile([P, BANK], F32, tag="bank", name="flipped%d" % a) for a in range(NODE_TILES)]
+            for q in range(BANK // P):
+                for a in range(NODE_TILES):
+                    nc.tensor.transpose(
+                        flipped[a][:, P * q : P * (q + 1)],
+                        source[:, (BANK // P) * half + q, P * a : P * (a + 1)],
+                        ident[:],
+                    )
+            return flipped
+
+        wi_q = quantise_weight(Wi, "wi")
+
+        x_sb = keep.tile([P, NODE_TILES, FEATURES], BF16)
+        nc.sync.dma_start(out=x_sb[:], in_=x.rearrange("(a p) k -> p a k", p=P))
+        x_words = x_sb[:].bitcast(F32)
+        x_grouped = keep.tile([P, PASSES, NODES, PACK], BF16, align_bytes=64)
+        for g in range(PASSES):
+            x_ps = psum.tile([P, 2, NODES], F32, tag="bank")
+            for u in range(2):
+                for a in range(NODE_TILES):
+                    nc.tensor.transpose(
+                        x_ps[:, u, P * a : P * (a + 1)],
+                        x_words[:, a, (K_PASS // 2) * g + u : (K_PASS // 2) * (g + 1) : 2],
+                        ident[:],
+                    )
+            nc.vector.tensor_copy(
+                out=x_grouped[:, g, :, :].bitcast(F32), in_=x_ps[:].rearrange("p u n -> p n u")
+            )
+        x_q = quantise_nodes(x_grouped, "x")
+
+        ui_q = quantise_weight(Ui, "ui")
+        wu_q = quantise_weight(Wu, "wu")
+
+        child_rows = child_h.rearrange("n c k -> (n c) k").rearrange(
+            "(l q s) k -> l q s k", q=P, s=ROWS_PER_PARTITION
+        )
+        loads_per_tile = CHILD_LOADS // NODE_TILES
+        h_grouped = keep.tile([P, PASSES, NODES, PACK], BF16, align_bytes=64)
+        for a in range(NODE_TILES):
+            h_ps = [
+                psum.tile([P, PACK, P], F32, tag="bank", name="h_ps%d" % g) for g in range(PASSES)
+            ]
+            for l in range(loads_per_tile):
+                child = child_pool.tile([P, ROWS_PER_PARTITION, FEATURES], BF16)
+                nc.sync.dma_start(out=child[:], in_=child_rows[loads_per_tile * a + l])
+                by_word = child[:].rearrange("q s (g p t) -> q s g t p", g=PASSES, t=PACK)
+                for g in range(PASSES):
+                    for t in range(PACK):
+                        for s in range(ROWS_PER_PARTITION):
+                            nc.tensor.matmul(
+                                out=h_ps[g][:, t, NODES_PER_LOAD * l : NODES_PER_LOAD * (l + 1)],
+                                lhsT=by_word[:, s, g, t, :],
+                                rhs=node_of[:],
+                                start=(s == 0),
+                                stop=(s == ROWS_PER_PARTITION - 1),
+                            )
+            for g in range(PASSES):
+                nc.vector.tensor_copy(
+                    out=h_grouped[:, g, P * a : P * (a + 1), :],
+                    in_=h_ps[g][:].rearrange("p t n -> p n t"),
+                )
+        h_q = quantise_nodes(h_grouped, "h")
+
+        uu_q = quantise_weight(Uu, "uu")
+        fc_sb = keep.tile([P, NODE_TILES, HIDDEN], BF16)
+        nc.sync.dma_start(out=fc_sb[:], in_=fc_sum.rearrange("(a p) n -> p a n", p=P))
+
+        i_gate = gate(GATE_I, wi_q, ui_q, ACT.Sigmoid, "i")
+        u_gate = gate(GATE_U, wu_q, uu_q, ACT.Tanh, "u")
+        iu = keep.tile([P, COL_TILES, NODES], F32)
+        c_sb = keep.tile([P, NODE_TILES, HIDDEN], F32)
+        tanh_c = keep.tile([P, NODE_TILES, HIDDEN], F32)
+        for half in range(HIDDEN // BANK):
+            tiles = slice((BANK // P) * half, (BANK // P) * (half + 1))
+            cols = slice(BANK * half, BANK * (half + 1))
+            nc.vector.tensor_tensor(
+                out=iu[:, tiles, :], in0=i_gate[:, tiles, :], in1=u_gate[:, tiles, :], op=ALU.mult
+            )
+            iu_flipped = flip_back(iu, half)
+            for a in range(NODE_TILES):
+                nc.vector.tensor_tensor(
+                    out=c_sb[:, a, cols], in0=iu_flipped[a][:], in1=fc_sb[:, a, cols], op=ALU.add
+                )
+                nc.scalar.activation(out=tanh_c[:, a, cols], in_=c_sb[:, a, cols], func=ACT.Tanh)
+                nc.sync.dma_start(out=out[1, P * a : P * (a + 1), cols], in_=c_sb[:, a, cols])
+
+        wo_q = quantise_weight(Wo, "wo")
+        uo_q = quantise_weight(Uo, "uo")
+        o_gate = gate(GATE_O, wo_q, uo_q, ACT.Sigmoid, "o")
+        h_sb = keep.tile([P, NODE_TILES, HIDDEN], F32)
+        for half in range(HIDDEN // BANK):
+            cols = slice(BANK * half, BANK * (half + 1))
+            o_flipped = flip_back(o_gate, half)
+            for a in range(NODE_TILES):
+                nc.vector.tensor_tensor(
+                    out=h_sb[:, a, cols], in0=o_flipped[a][:], in1=tanh_c[:, a, cols], op=ALU.mult
+                )
+                nc.sync.dma_start(out=out[0, P * a : P * (a + 1), cols], in_=h_sb[:, a, cols])

@@ -22,15 +22,14 @@ PASSES = FEATURES // K_PASS
 HIDDEN = 1024
 COL_TILES = HIDDEN // P
 BANK = 512
+HALF = HIDDEN // 2
+TILES_PER_HALF = HALF // P
 
 ROWS_PER_PARTITION = 4
-NODES_PER_LOAD = P * ROWS_PER_PARTITION // CHILDREN
-PARTITIONS_PER_NODE = P // NODES_PER_LOAD
-CHILD_LOADS = NODES // NODES_PER_LOAD
+PAIR = CHILDREN // ROWS_PER_PARTITION
+NODES_PER_LOAD = P // PAIR
 
 GATE_I, GATE_U, GATE_O = 0, 1, 2
-
-VECTOR_COLS = 512
 
 FLOPS = 2 * NODES * FEATURES * HIDDEN * 6
 
@@ -40,209 +39,343 @@ def tile_childsumtreelstmcell_pb_kernel(
 ):
     nc = tc.nc
     with ExitStack() as ctx:
+        ctx.enter_context(tc.manual_schedule())
         const = ctx.enter_context(tc.tile_pool(name="const", bufs=1))
         keep = ctx.enter_context(tc.tile_pool(name="keep", bufs=1))
-        raw_pool = ctx.enter_context(tc.tile_pool(name="raw", bufs=5))
-        grouped_pool = ctx.enter_context(tc.tile_pool(name="grouped", bufs=3))
+        raw_pool = ctx.enter_context(tc.tile_pool(name="raw", bufs=6))
+        grouped_pool = ctx.enter_context(tc.tile_pool(name="grouped", bufs=6))
         child_pool = ctx.enter_context(tc.tile_pool(name="child", bufs=4))
         psum = ctx.enter_context(tc.psum_pool(name="psum", bufs=8))
 
         ident = const.tile([P, P], F32)
         make_identity(nc, ident[:])
-        node_of_f32 = const.tile([P, NODES_PER_LOAD], F32)
+        pair_sum_f32 = const.tile([P, P // PAIR], F32)
         nc.vector.reduce_sum(
-            out=node_of_f32[:],
-            in_=ident[:].rearrange("q (i r) -> q i r", r=PARTITIONS_PER_NODE),
-            axis=mybir.AxisListType.X,
+            out=pair_sum_f32[:], in_=ident[:].rearrange("q (i r) -> q i r", r=PAIR), axis=mybir.AxisListType.X
         )
-        node_of = const.tile([P, NODES_PER_LOAD], BF16)
-        nc.vector.tensor_copy(out=node_of[:], in_=node_of_f32[:])
+        pair_sum = const.tile([P, P // PAIR], BF16)
+        nc.vector.tensor_copy(out=pair_sum[:], in_=pair_sum_f32[:])
 
         zero_col = const.tile([P, 1], F32)
         nc.vector.memset(zero_col[:], 0.0)
         half_col = const.tile([P, 1], F32)
         nc.scalar.activation(out=half_col[:], in_=zero_col[:], func=ACT.Sigmoid)
 
-        gate_biases = ((bWi, bUi), (bWu, bUu), (bWo, bUo))
         bias_rows = const.tile([P, P], BF16)
         nc.vector.memset(bias_rows[:], 0.0)
-        rows_per_gate = PARTITIONS_PER_NODE * COL_TILES
-        for m, pair_of_biases in enumerate(gate_biases):
-            for r, b in enumerate(pair_of_biases):
-                nc.scalar.dma_start(
-                    out=bias_rows[rows_per_gate * m + r : rows_per_gate * (m + 1) : PARTITIONS_PER_NODE, :],
-                    in_=b.rearrange("(j p) -> j p", p=P),
-                )
-        bias_ps = psum.tile([P, NODES_PER_LOAD], F32, tag="bank")
-        nc.tensor.matmul(out=bias_ps[:], lhsT=bias_rows[:], rhs=node_of[:], start=True, stop=True)
-        bias = const.tile([P, NODES_PER_LOAD], F32)
-        nc.vector.tensor_copy(out=bias[:], in_=bias_ps[:])
+        bias = const.tile([P, P // PAIR], F32)
 
-        def quantise_weight(w, label):
-            quantised = []
-            for g in range(PASSES):
-                raw = raw_pool.tile([P, PACK, HIDDEN], BF16)
-                nc.sync.dma_start(
-                    out=raw[:],
-                    in_=w[K_PASS * g : K_PASS * (g + 1), :].rearrange("(p t) n -> p t n", t=PACK),
-                )
-                grouped = grouped_pool.tile([P, HIDDEN, PACK], BF16, align_bytes=64)
-                for copy, cols in (
-                    (nc.vector.tensor_copy, slice(0, VECTOR_COLS)),
-                    (nc.scalar.copy, slice(VECTOR_COLS, HIDDEN)),
-                ):
-                    copy(
-                        out=grouped[:, cols, :].rearrange("p (c i) t -> p c t i", i=4),
-                        in_=raw[:, :, cols].rearrange("p t (c i) -> p c t i", i=4),
-                    )
-                words = keep.tile([P, HIDDEN], U32, align_bytes=64, name="words_%s%d" % (label, g))
-                scales = keep.tile([P, HIDDEN], U8, align_bytes=64, name="scales_%s%d" % (label, g))
-                for cols in (slice(0, HIDDEN // 2), slice(HIDDEN // 2, HIDDEN)):
-                    nc.vector.quantize_mx(
-                        out=words[:, cols].bitcast(FP8X4),
-                        scales=scales[:, cols],
-                        in_=grouped[:, cols, :].rearrange("p n t -> p (n t)"),
-                    )
-                quantised.append((words, scales))
-            return quantised
+        bias_vectors = [(m, r, b) for m, pair in enumerate(((bWi, bUi), (bWu, bUu), (bWo, bUo))) for r, b in enumerate(pair)]
 
-        def quantise_nodes(grouped, label):
-            words = keep.tile([P, PASSES, NODES], U32, align_bytes=64, name="words_" + label)
-            scales = keep.tile([P, PASSES, NODES], U8, align_bytes=64, name="scales_" + label)
-            nc.vector.quantize_mx(
-                out=words[:].rearrange("p g n -> p (g n)").bitcast(FP8X4),
-                scales=scales[:].rearrange("p g n -> p (g n)"),
-                in_=grouped[:].rearrange("p g n t -> p (g n t)"),
+        def load_bias():
+            m, r, b = bias_vectors.pop()
+            first = PAIR * COL_TILES * m + r
+            nc.sync.dma_start(
+                out=bias_rows[first : PAIR * COL_TILES * (m + 1) : PAIR, :],
+                in_=b.rearrange("(j p) -> j p", p=P),
             )
-            return words, scales
 
-        def gate(m, w_q, u_q, func, label):
-            result = keep.tile([P, COL_TILES, NODES], F32, name="gate_" + label)
-            acc = [psum.tile([P, NODES], F32, tag="bank", name="acc%d" % j) for j in range(COL_TILES)]
+        def sum_biases():
+            bias_ps = psum.tile([P, P // PAIR], F32, tag="bank")
+            nc.tensor.matmul(out=bias_ps[:], lhsT=bias_rows[:], rhs=pair_sum[:], start=True, stop=True)
+            nc.vector.tensor_copy(out=bias[:], in_=bias_ps[:])
 
-            def mx_pass(j, weight_q, nodes_q, g, start, stop):
-                (w_words, w_scales), (a_words, a_scales) = weight_q[g], nodes_q
-                cols = slice(P * j, P * (j + 1))
-                nc.tensor.matmul_mx(
-                    out=acc[j][:],
-                    lhsT=w_words[:, cols].bitcast(FP8X4),
-                    lhsT_scale=w_scales[:, cols],
-                    rhs=a_words[:, g, :].bitcast(FP8X4),
-                    rhs_scale=a_scales[:, g, :],
-                    start=start,
-                    stop=stop,
+        weights = {"wi": Wi, "ui": Ui, "wu": Wu, "uu": Uu, "wo": Wo, "uo": Uo}
+        raws, words, scales, regrouped = {}, {}, {}, {}
+
+        def load_weight(label, g, pieces=1):
+            raw = raw_pool.tile([P, PACK, HIDDEN], BF16, name="raw")
+            rows = weights[label][K_PASS * g : K_PASS * (g + 1), :].rearrange("(p t) n -> p t n", t=PACK)
+            width = HIDDEN // pieces
+            for c in range(pieces):
+                cols = slice(width * c, width * (c + 1))
+                nc.sync.dma_start(out=raw[:, :, cols], in_=rows[:, :, cols])
+            raws[label, g] = raw
+            words[label, g] = keep.tile([P, HIDDEN], U32, align_bytes=64, name="words_%s%d" % (label, g))
+            scales[label, g] = keep.tile([P, HIDDEN], U8, align_bytes=64, name="scales_%s%d" % (label, g))
+
+        def regroup(copy, label, g, first, end):
+            half = first // HALF
+            if (label, g, half) not in regrouped:
+                regrouped[label, g, half] = grouped_pool.tile([P, HALF, PACK], BF16, align_bytes=64, name="grouped")
+            copy(
+                out=regrouped[label, g, half][:, first - HALF * half : end - HALF * half, :].rearrange(
+                    "p (c i) t -> p c t i", i=4
+                ),
+                in_=raws[label, g][:, :, first:end].rearrange("p t (c i) -> p c t i", i=4),
+            )
+
+        def quantise(label, g, half):
+            cols = slice(HALF * half, HALF * (half + 1))
+            nc.vector.quantize_mx(
+                out=words[label, g][:, cols].bitcast(FP8X4),
+                scales=scales[label, g][:, cols],
+                in_=regrouped[label, g, half][:].rearrange("p n t -> p (n t)"),
+            )
+
+        def load_child():
+            child = child_pool.tile([P, ROWS_PER_PARTITION, FEATURES], BF16, name="child")
+            nc.sync.dma_start(out=child[:], in_=child_rows[len(children)])
+            children.append(child)
+
+        def sum_children(l):
+            by_word = children[l][:].rearrange("q s (g p t) -> q s g t p", g=PASSES, t=PACK)
+            h_ps = psum.tile([P, PASSES, PACK, NODES_PER_LOAD], F32, tag="bank", name="h_ps")
+            for g in range(PASSES):
+                for t in range(PACK):
+                    for s in range(ROWS_PER_PARTITION):
+                        nc.tensor.matmul(
+                            out=h_ps[:, g, t, :],
+                            lhsT=by_word[:, s, g, t, :],
+                            rhs=pair_sum[:],
+                            start=(s == 0),
+                            stop=(s == ROWS_PER_PARTITION - 1),
+                        )
+            return h_ps
+
+        def interleave_sums(h_ps, l):
+            first = NODES_PER_LOAD * l
+            nc.vector.tensor_copy(
+                out=h_grouped[:, :, first : first + NODES_PER_LOAD, :],
+                in_=h_ps[:].rearrange("p g t n -> p g n t"),
+            )
+
+        def quantise_nodes(operand, grouped, first, end):
+            node_words, node_scales = operand
+            for g in range(PASSES):
+                nc.vector.quantize_mx(
+                    out=node_words[:, g, first:end].bitcast(FP8X4),
+                    scales=node_scales[:, g, first:end],
+                    in_=grouped[:, g, first:end, :].rearrange("p n t -> p (n t)"),
                 )
 
+        def mx_pass(acc, key, operand, first=False, last=False):
+            label, g, half = key
+            node_words, node_scales = operand
+            for q in range(TILES_PER_HALF):
+                cols = slice(HALF * half + P * q, HALF * half + P * (q + 1))
+                nc.tensor.matmul_mx(
+                    out=acc[q][:],
+                    lhsT=words[label, g][:, cols].bitcast(FP8X4),
+                    lhsT_scale=scales[label, g][:, cols],
+                    rhs=node_words[:, g, :].bitcast(FP8X4),
+                    rhs_scale=node_scales[:, g, :],
+                    start=first,
+                    stop=last,
+                )
+
+        def open_gate(w, half):
+            acc = [psum.tile([P, NODES], F32, tag="bank", name="acc") for q in range(TILES_PER_HALF)]
             for g in range(PASSES):
-                for j in range(COL_TILES):
-                    mx_pass(j, w_q, x_q, g, g == 0, False)
-            for j in range(COL_TILES):
-                for g in range(PASSES):
-                    mx_pass(j, u_q, h_q, g, False, g == PASSES - 1)
+                mx_pass(acc, (w, g, half), x_q, first=(g == 0))
+            return acc
+
+        def activate(acc, m, func, half, result):
+            for q in range(TILES_PER_HALF):
+                j = TILES_PER_HALF * half + q
                 nc.scalar.activation(
                     out=result[:, j, :],
-                    in_=acc[j][:],
+                    in_=acc[q][:],
                     func=func,
                     bias=bias[:, COL_TILES * m + j : COL_TILES * m + j + 1],
                 )
-            return result
 
-        def flip_back(source, half):
-            flipped = [psum.tile([P, BANK], F32, tag="bank", name="flipped%d" % a) for a in range(NODE_TILES)]
-            for q in range(BANK // P):
-                for a in range(NODE_TILES):
-                    nc.tensor.transpose(
-                        flipped[a][:, P * q : P * (q + 1)],
-                        source[:, (BANK // P) * half + q, P * a : P * (a + 1)],
-                        ident[:],
+        def gate_tile(m, w, u, func, half, a, result):
+            acc = psum.tile([P, TILES_PER_HALF, P], F32, tag="bank", name="acc_tile")
+            nodes = slice(P * a, P * (a + 1))
+            passes = [(label, g, operand) for label, operand in ((w, x_q), (u, h_q)) for g in range(PASSES)]
+            for q in range(TILES_PER_HALF):
+                cols = slice(HALF * half + P * q, HALF * half + P * (q + 1))
+                for n, (label, g, (node_words, node_scales)) in enumerate(passes):
+                    nc.tensor.matmul_mx(
+                        out=acc[:, q, :],
+                        lhsT=words[label, g][:, cols].bitcast(FP8X4),
+                        lhsT_scale=scales[label, g][:, cols],
+                        rhs=node_words[:, g, nodes].bitcast(FP8X4),
+                        rhs_scale=node_scales[:, g, nodes],
+                        start=(n == 0),
+                        stop=(n == len(passes) - 1),
                     )
+            for q in range(TILES_PER_HALF):
+                j = TILES_PER_HALF * half + q
+                nc.scalar.activation(
+                    out=result[:, j, nodes],
+                    in_=acc[:, q, :],
+                    func=func,
+                    bias=bias[:, COL_TILES * m + j : COL_TILES * m + j + 1],
+                )
+
+        def flip_back(source, half, a):
+            flipped = psum.tile([P, BANK], F32, tag="bank", name="flipped")
+            for q in range(TILES_PER_HALF):
+                nc.tensor.transpose(
+                    flipped[:, P * q : P * (q + 1)],
+                    source[:, TILES_PER_HALF * half + q, P * a : P * (a + 1)],
+                    ident[:],
+                )
             return flipped
 
-        wi_q = quantise_weight(Wi, "wi")
+        def multiply_gates(half, a):
+            tiles = slice(TILES_PER_HALF * half, TILES_PER_HALF * (half + 1))
+            nodes = slice(P * a, P * (a + 1))
+            nc.vector.tensor_tensor(
+                out=u_gate[:, tiles, nodes], in0=i_gate[:, tiles, nodes], in1=u_gate[:, tiles, nodes], op=ALU.mult
+            )
 
-        x_sb = keep.tile([P, NODE_TILES, FEATURES], BF16)
-        nc.sync.dma_start(out=x_sb[:], in_=x.rearrange("(a p) k -> p a k", p=P))
-        x_words = x_sb[:].bitcast(F32)
-        x_grouped = keep.tile([P, PASSES, NODES, PACK], BF16, align_bytes=64)
-        for g in range(PASSES):
-            x_ps = psum.tile([P, 2, NODES], F32, tag="bank")
-            for u in range(2):
-                for a in range(NODE_TILES):
+        def cell_state(iu_flipped, half, a):
+            cols = slice(HALF * half, HALF * (half + 1))
+            nc.vector.tensor_tensor(
+                out=c_sb[:, a, cols], in0=iu_flipped[:], in1=fc_sb[:, a, cols], op=ALU.add
+            )
+            nc.scalar.activation(out=tanh_c[:, a, cols], in_=c_sb[:, a, cols], func=ACT.Tanh)
+            nc.sync.dma_start(out=out[1, P * a : P * (a + 1), cols], in_=c_sb[:, a, cols])
+
+        def hidden_state(o_flipped, half, a):
+            cols = slice(HALF * half, HALF * (half + 1))
+            nc.vector.tensor_tensor(
+                out=tanh_c[:, a, cols], in0=o_flipped[:], in1=tanh_c[:, a, cols], op=ALU.mult
+            )
+            nc.sync.dma_start(out=out[0, P * a : P * (a + 1), cols], in_=tanh_c[:, a, cols])
+
+        def interleave_x(a):
+            x_ps = psum.tile([P, PASSES, 2, P], F32, tag="bank")
+            for g in range(PASSES):
+                for u in range(2):
                     nc.tensor.transpose(
-                        x_ps[:, u, P * a : P * (a + 1)],
+                        x_ps[:, g, u, :],
                         x_words[:, a, (K_PASS // 2) * g + u : (K_PASS // 2) * (g + 1) : 2],
                         ident[:],
                     )
             nc.vector.tensor_copy(
-                out=x_grouped[:, g, :, :].bitcast(F32), in_=x_ps[:].rearrange("p u n -> p n u")
+                out=x_grouped[:, :, P * a : P * (a + 1), :].bitcast(F32), in_=x_ps[:].rearrange("p g u n -> p g n u")
             )
-        x_q = quantise_nodes(x_grouped, "x")
-
-        ui_q = quantise_weight(Ui, "ui")
-        wu_q = quantise_weight(Wu, "wu")
 
         child_rows = child_h.rearrange("n c k -> (n c) k").rearrange(
             "(l q s) k -> l q s k", q=P, s=ROWS_PER_PARTITION
         )
-        loads_per_tile = CHILD_LOADS // NODE_TILES
+        children = []
+        node_operands = []
+        for label in ("x", "h"):
+            node_words = keep.tile([P, PASSES, NODES], U32, align_bytes=64, name="words_" + label)
+            node_scales = keep.tile([P, PASSES, NODES], U8, align_bytes=64, name="scales_" + label)
+            node_operands.append((node_words, node_scales))
+        x_q, h_q = node_operands
+        x_sb = keep.tile([P, NODE_TILES, FEATURES], BF16)
+        x_words = x_sb[:].bitcast(F32)
+        x_grouped = keep.tile([P, PASSES, NODES, PACK], BF16, align_bytes=64)
         h_grouped = keep.tile([P, PASSES, NODES, PACK], BF16, align_bytes=64)
-        for a in range(NODE_TILES):
-            h_ps = [
-                psum.tile([P, PACK, P], F32, tag="bank", name="h_ps%d" % g) for g in range(PASSES)
-            ]
-            for l in range(loads_per_tile):
-                child = child_pool.tile([P, ROWS_PER_PARTITION, FEATURES], BF16)
-                nc.sync.dma_start(out=child[:], in_=child_rows[loads_per_tile * a + l])
-                by_word = child[:].rearrange("q s (g p t) -> q s g t p", g=PASSES, t=PACK)
-                for g in range(PASSES):
-                    for t in range(PACK):
-                        for s in range(ROWS_PER_PARTITION):
-                            nc.tensor.matmul(
-                                out=h_ps[g][:, t, NODES_PER_LOAD * l : NODES_PER_LOAD * (l + 1)],
-                                lhsT=by_word[:, s, g, t, :],
-                                rhs=node_of[:],
-                                start=(s == 0),
-                                stop=(s == ROWS_PER_PARTITION - 1),
-                            )
-            for g in range(PASSES):
-                nc.vector.tensor_copy(
-                    out=h_grouped[:, g, P * a : P * (a + 1), :],
-                    in_=h_ps[g][:].rearrange("p t n -> p n t"),
-                )
-        h_q = quantise_nodes(h_grouped, "h")
-
-        uu_q = quantise_weight(Uu, "uu")
         fc_sb = keep.tile([P, NODE_TILES, HIDDEN], BF16)
-        nc.sync.dma_start(out=fc_sb[:], in_=fc_sum.rearrange("(a p) n -> p a n", p=P))
-
-        i_gate = gate(GATE_I, wi_q, ui_q, ACT.Sigmoid, "i")
-        u_gate = gate(GATE_U, wu_q, uu_q, ACT.Tanh, "u")
-        iu = keep.tile([P, COL_TILES, NODES], F32)
+        i_gate = keep.tile([P, COL_TILES, NODES], F32)
+        u_gate = keep.tile([P, COL_TILES, NODES], F32)
+        o_gate = keep.tile([P, COL_TILES, NODES], F32)
         c_sb = keep.tile([P, NODE_TILES, HIDDEN], F32)
         tanh_c = keep.tile([P, NODE_TILES, HIDDEN], F32)
-        for half in range(HIDDEN // BANK):
-            tiles = slice((BANK // P) * half, (BANK // P) * (half + 1))
-            cols = slice(BANK * half, BANK * (half + 1))
-            nc.vector.tensor_tensor(
-                out=iu[:, tiles, :], in0=i_gate[:, tiles, :], in1=u_gate[:, tiles, :], op=ALU.mult
-            )
-            iu_flipped = flip_back(iu, half)
-            for a in range(NODE_TILES):
-                nc.vector.tensor_tensor(
-                    out=c_sb[:, a, cols], in0=iu_flipped[a][:], in1=fc_sb[:, a, cols], op=ALU.add
-                )
-                nc.scalar.activation(out=tanh_c[:, a, cols], in_=c_sb[:, a, cols], func=ACT.Tanh)
-                nc.sync.dma_start(out=out[1, P * a : P * (a + 1), cols], in_=c_sb[:, a, cols])
+        vcopy, scopy = nc.vector.tensor_copy, nc.scalar.copy
 
-        wo_q = quantise_weight(Wo, "wo")
-        uo_q = quantise_weight(Uo, "uo")
-        o_gate = gate(GATE_O, wo_q, uo_q, ACT.Sigmoid, "o")
-        h_sb = keep.tile([P, NODE_TILES, HIDDEN], F32)
-        for half in range(HIDDEN // BANK):
-            cols = slice(BANK * half, BANK * (half + 1))
-            o_flipped = flip_back(o_gate, half)
-            for a in range(NODE_TILES):
-                nc.vector.tensor_tensor(
-                    out=h_sb[:, a, cols], in0=o_flipped[a][:], in1=tanh_c[:, a, cols], op=ALU.mult
-                )
-                nc.sync.dma_start(out=out[0, P * a : P * (a + 1), cols], in_=h_sb[:, a, cols])
+        load_weight("wi", 0, pieces=4)
+        load_weight("wi", 1)
+        load_bias()
+        nc.sync.dma_start(out=x_sb[:], in_=x.rearrange("(a p) k -> p a k", p=P))
+        load_bias()
+        for label, g in (("ui", 0), ("ui", 1), ("wu", 0), ("wu", 1)):
+            load_weight(label, g)
+            load_bias()
+
+        for half in range(2):
+            regroup(vcopy, "wi", 0, HALF * half, HALF * half + HALF // 2)
+            regroup(scopy, "wi", 0, HALF * half + HALF // 2, HALF * (half + 1))
+
+        def weight_pass(label, g, before):
+            regroup(vcopy, label, g, 0, HALF)
+            regroup(scopy, label, g, HALF, HIDDEN)
+            quantise(before[0], before[1], 1)
+            quantise(label, g, 0)
+
+        load_weight("uu", 0)
+        quantise("wi", 0, 0)
+        weight_pass("wi", 1, ("wi", 0))
+        load_weight("uu", 1)
+        load_child()
+        load_child()
+        nc.sync.dma_start(out=fc_sb[:], in_=fc_sum.rearrange("(a p) n -> p a n", p=P))
+        for a in range(NODE_TILES):
+            interleave_x(a)
+        weight_pass("ui", 0, ("wi", 1))
+        load_weight("wo", 0)
+        quantise_nodes(x_q, x_grouped, 0, NODES)
+        weight_pass("ui", 1, ("ui", 0))
+        load_weight("wo", 1)
+        load_child()
+        load_child()
+        weight_pass("wu", 0, ("ui", 1))
+        load_weight("uo", 0)
+        sum_biases()
+        weight_pass("wu", 1, ("wu", 0))
+        load_weight("uo", 1)
+        weight_pass("uu", 0, ("wu", 1))
+        weight_pass("uu", 1, ("uu", 0))
+        quantise("uu", 1, 1)
+        Q = HALF // 2
+        for l in range(2):
+            interleave_sums(sum_children(l), l)
+        quantise_nodes(h_q, h_grouped, 0, P)
+        regroup(vcopy, "wo", 0, 0, HALF)
+        gate_tile(GATE_I, "wi", "ui", ACT.Sigmoid, 0, 0, i_gate)
+        regroup(scopy, "wo", 0, HALF, HALF + Q)
+        gate_tile(GATE_U, "wu", "uu", ACT.Tanh, 0, 0, u_gate)
+        regroup(scopy, "wo", 0, HALF + Q, HIDDEN)
+        gate_tile(GATE_I, "wi", "ui", ACT.Sigmoid, 1, 0, i_gate)
+        gate_tile(GATE_U, "wu", "uu", ACT.Tanh, 1, 0, u_gate)
+        quantise("wo", 0, 0)
+        multiply_gates(0, 0)
+        flipped = [flip_back(u_gate, 0, 0)]
+        regroup(vcopy, "wo", 1, 0, HALF)
+        multiply_gates(1, 0)
+        flipped.append(flip_back(u_gate, 1, 0))
+        regroup(scopy, "wo", 1, HALF, HALF + Q)
+        cell_state(flipped[0], 0, 0)
+        quantise("wo", 1, 0)
+        regroup(scopy, "wo", 1, HALF + Q, HIDDEN)
+        cell_state(flipped[1], 1, 0)
+        quantise("wo", 0, 1)
+        o_acc = open_gate("wo", 0)
+
+        V = 320
+        def share(g, half):
+            regroup(vcopy, "uo", g, HALF * half, HALF * half + V)
+            regroup(scopy, "uo", g, HALF * half + V, HALF * (half + 1))
+
+        for l in (2, 3):
+            interleave_sums(sum_children(l), l)
+        quantise_nodes(h_q, h_grouped, P, NODES)
+        share(0, 0)
+        quantise("wo", 1, 1)
+        share(0, 1)
+        gate_tile(GATE_I, "wi", "ui", ACT.Sigmoid, 0, 1, i_gate)
+        gate_tile(GATE_U, "wu", "uu", ACT.Tanh, 0, 1, u_gate)
+        quantise("uo", 0, 0)
+        multiply_gates(0, 1)
+        quantise("uo", 0, 1)
+        share(1, 0)
+        gate_tile(GATE_I, "wi", "ui", ACT.Sigmoid, 1, 1, i_gate)
+        flipped = flip_back(u_gate, 0, 1)
+        gate_tile(GATE_U, "wu", "uu", ACT.Tanh, 1, 1, u_gate)
+        cell_state(flipped, 0, 1)
+        quantise("uo", 1, 0)
+        multiply_gates(1, 1)
+        share(1, 1)
+        mx_pass(o_acc, ("uo", 0, 0), h_q)
+        mx_pass(o_acc, ("uo", 1, 0), h_q, last=True)
+        flipped = flip_back(u_gate, 1, 1)
+        activate(o_acc, GATE_O, ACT.Sigmoid, 0, o_gate)
+        cell_state(flipped, 1, 1)
+        quantise("uo", 1, 1)
+        o_acc = open_gate("wo", 1)
+        mx_pass(o_acc, ("uo", 0, 1), h_q)
+        mx_pass(o_acc, ("uo", 1, 1), h_q, last=True)
+        flipped = [flip_back(o_gate, 0, a) for a in range(NODE_TILES)]
+        activate(o_acc, GATE_O, ACT.Sigmoid, 1, o_gate)
+        for a in range(NODE_TILES):
+            hidden_state(flipped[a], 0, a)
+        for a in range(NODE_TILES):
+            hidden_state(flip_back(o_gate, 1, a), 1, a)

@@ -100,9 +100,9 @@ def tile_childsumtreelstmcell_pb_kernel(
                 regrouped[label, g, half] = grouped_pool.tile([P, HALF, PACK], BF16, align_bytes=64, name="grouped")
             copy(
                 out=regrouped[label, g, half][:, first - HALF * half : end - HALF * half, :].rearrange(
-                    "p (c i) t -> p c t i", i=4
+                    "p (c i) t -> p c t i", i=8
                 ),
-                in_=raws[label, g][:, :, first:end].rearrange("p t (c i) -> p c t i", i=4),
+                in_=raws[label, g][:, :, first:end].rearrange("p t (c i) -> p c t i", i=8),
             )
 
         def quantise(label, g, half):
@@ -133,9 +133,9 @@ def tile_childsumtreelstmcell_pb_kernel(
                         )
             return h_ps
 
-        def interleave_sums(h_ps, l):
+        def interleave_sums(copy, h_ps, l):
             first = NODES_PER_LOAD * l
-            nc.vector.tensor_copy(
+            copy(
                 out=h_grouped[:, :, first : first + NODES_PER_LOAD, :],
                 in_=h_ps[:].rearrange("p g t n -> p g n t"),
             )
@@ -237,7 +237,7 @@ def tile_childsumtreelstmcell_pb_kernel(
             )
             nc.sync.dma_start(out=out[0, P * a : P * (a + 1), cols], in_=tanh_c[:, a, cols])
 
-        def interleave_x(a):
+        def interleave_x(copy, a):
             x_ps = psum.tile([P, PASSES, 2, P], F32, tag="bank")
             for g in range(PASSES):
                 for u in range(2):
@@ -246,7 +246,7 @@ def tile_childsumtreelstmcell_pb_kernel(
                         x_words[:, a, (K_PASS // 2) * g + u : (K_PASS // 2) * (g + 1) : 2],
                         ident[:],
                     )
-            nc.vector.tensor_copy(
+            copy(
                 out=x_grouped[:, :, P * a : P * (a + 1), :].bitcast(F32), in_=x_ps[:].rearrange("p g u n -> p g n u")
             )
 
@@ -297,9 +297,8 @@ def tile_childsumtreelstmcell_pb_kernel(
         load_weight("uu", 1)
         load_child()
         load_child()
-        nc.sync.dma_start(out=fc_sb[:], in_=fc_sum.rearrange("(a p) n -> p a n", p=P))
         for a in range(NODE_TILES):
-            interleave_x(a)
+            interleave_x(scopy, a)
         weight_pass("ui", 0, ("wi", 1))
         load_weight("wo", 0)
         quantise_nodes(x_q, x_grouped, 0, NODES)
@@ -307,6 +306,7 @@ def tile_childsumtreelstmcell_pb_kernel(
         load_weight("wo", 1)
         load_child()
         load_child()
+        nc.sync.dma_start(out=fc_sb[:], in_=fc_sum.rearrange("(a p) n -> p a n", p=P))
         weight_pass("wu", 0, ("ui", 1))
         load_weight("uo", 0)
         sum_biases()
@@ -317,7 +317,7 @@ def tile_childsumtreelstmcell_pb_kernel(
         quantise("uu", 1, 1)
         Q = HALF // 2
         for l in range(2):
-            interleave_sums(sum_children(l), l)
+            interleave_sums(scopy, sum_children(l), l)
         quantise_nodes(h_q, h_grouped, 0, P)
         regroup(vcopy, "wo", 0, 0, HALF)
         gate_tile(GATE_I, "wi", "ui", ACT.Sigmoid, 0, 0, i_gate)
@@ -327,27 +327,28 @@ def tile_childsumtreelstmcell_pb_kernel(
         gate_tile(GATE_I, "wi", "ui", ACT.Sigmoid, 1, 0, i_gate)
         gate_tile(GATE_U, "wu", "uu", ACT.Tanh, 1, 0, u_gate)
         quantise("wo", 0, 0)
-        multiply_gates(0, 0)
-        flipped = [flip_back(u_gate, 0, 0)]
         regroup(vcopy, "wo", 1, 0, HALF)
+        multiply_gates(0, 0)
+        h_ps = [sum_children(2)]
+        flipped = [flip_back(u_gate, 0, 0)]
         multiply_gates(1, 0)
         flipped.append(flip_back(u_gate, 1, 0))
+        h_ps.append(sum_children(3))
         regroup(scopy, "wo", 1, HALF, HALF + Q)
+        interleave_sums(vcopy, h_ps[0], 2)
         cell_state(flipped[0], 0, 0)
         quantise("wo", 1, 0)
+        interleave_sums(vcopy, h_ps[1], 3)
+        quantise_nodes(h_q, h_grouped, P, NODES)
         regroup(scopy, "wo", 1, HALF + Q, HIDDEN)
         cell_state(flipped[1], 1, 0)
         quantise("wo", 0, 1)
-        o_acc = open_gate("wo", 0)
+        V = 352
 
-        V = 320
         def share(g, half):
             regroup(vcopy, "uo", g, HALF * half, HALF * half + V)
             regroup(scopy, "uo", g, HALF * half + V, HALF * (half + 1))
 
-        for l in (2, 3):
-            interleave_sums(sum_children(l), l)
-        quantise_nodes(h_q, h_grouped, P, NODES)
         share(0, 0)
         quantise("wo", 1, 1)
         share(0, 1)
@@ -358,12 +359,13 @@ def tile_childsumtreelstmcell_pb_kernel(
         quantise("uo", 0, 1)
         share(1, 0)
         gate_tile(GATE_I, "wi", "ui", ACT.Sigmoid, 1, 1, i_gate)
-        flipped = flip_back(u_gate, 0, 1)
         gate_tile(GATE_U, "wu", "uu", ACT.Tanh, 1, 1, u_gate)
+        flipped = flip_back(u_gate, 0, 1)
         cell_state(flipped, 0, 1)
         quantise("uo", 1, 0)
         multiply_gates(1, 1)
         share(1, 1)
+        o_acc = open_gate("wo", 0)
         mx_pass(o_acc, ("uo", 0, 0), h_q)
         mx_pass(o_acc, ("uo", 1, 0), h_q, last=True)
         flipped = flip_back(u_gate, 1, 1)

@@ -105,12 +105,12 @@ def tile_childsumtreelstmcell_pb_kernel(
                 in_=raws[label, g][:, :, first:end].rearrange("p t (c i) -> p c t i", i=8),
             )
 
-        def quantise(label, g, half):
-            cols = slice(HALF * half, HALF * (half + 1))
+        def quantise(label, g, half, first=0, end=HALF):
+            cols = slice(HALF * half + first, HALF * half + end)
             nc.vector.quantize_mx(
                 out=words[label, g][:, cols].bitcast(FP8X4),
                 scales=scales[label, g][:, cols],
-                in_=regrouped[label, g, half][:].rearrange("p n t -> p (n t)"),
+                in_=regrouped[label, g, half][:, first:end, :].rearrange("p n t -> p (n t)"),
             )
 
         def load_child():
@@ -149,10 +149,10 @@ def tile_childsumtreelstmcell_pb_kernel(
                     in_=grouped[:, g, first:end, :].rearrange("p n t -> p (n t)"),
                 )
 
-        def mx_pass(acc, key, operand, first=False, last=False):
+        def mx_pass(acc, key, operand, first=False, last=False, tiles=range(TILES_PER_HALF)):
             label, g, half = key
             node_words, node_scales = operand
-            for q in range(TILES_PER_HALF):
+            for q in tiles:
                 cols = slice(HALF * half + P * q, HALF * half + P * (q + 1))
                 nc.tensor.matmul_mx(
                     out=acc[q][:],
@@ -170,8 +170,8 @@ def tile_childsumtreelstmcell_pb_kernel(
                 mx_pass(acc, (w, g, half), x_q, first=(g == 0))
             return acc
 
-        def activate(acc, m, func, half, result):
-            for q in range(TILES_PER_HALF):
+        def activate(acc, m, func, half, result, tiles=range(TILES_PER_HALF)):
+            for q in tiles:
                 j = TILES_PER_HALF * half + q
                 nc.scalar.activation(
                     out=result[:, j, :],
@@ -205,11 +205,11 @@ def tile_childsumtreelstmcell_pb_kernel(
                     bias=bias[:, COL_TILES * m + j : COL_TILES * m + j + 1],
                 )
 
-        def flip_back(source, half, a):
-            flipped = psum.tile([P, BANK], F32, tag="bank", name="flipped")
-            for q in range(TILES_PER_HALF):
+        def flip_back(source, half, a, tiles=range(TILES_PER_HALF)):
+            flipped = psum.tile([P, P * len(tiles)], F32, tag="bank", name="flipped")
+            for n, q in enumerate(tiles):
                 nc.tensor.transpose(
-                    flipped[:, P * q : P * (q + 1)],
+                    flipped[:, P * n : P * (n + 1)],
                     source[:, TILES_PER_HALF * half + q, P * a : P * (a + 1)],
                     ident[:],
                 )
@@ -230,8 +230,9 @@ def tile_childsumtreelstmcell_pb_kernel(
             nc.scalar.activation(out=tanh_c[:, a, cols], in_=c_sb[:, a, cols], func=ACT.Tanh)
             nc.sync.dma_start(out=out[1, P * a : P * (a + 1), cols], in_=c_sb[:, a, cols])
 
-        def hidden_state(o_flipped, half, a):
-            cols = slice(HALF * half, HALF * (half + 1))
+        def hidden_state(half, a, tiles=range(TILES_PER_HALF)):
+            o_flipped = flip_back(o_gate, half, a, tiles)
+            cols = slice(HALF * half + P * tiles[0], HALF * half + P * (tiles[-1] + 1))
             nc.vector.tensor_tensor(
                 out=tanh_c[:, a, cols], in0=o_flipped[:], in1=tanh_c[:, a, cols], op=ALU.mult
             )
@@ -294,9 +295,9 @@ def tile_childsumtreelstmcell_pb_kernel(
         load_weight("uu", 0)
         quantise("wi", 0, 0)
         weight_pass("wi", 1, ("wi", 0))
+        load_child()
+        load_child()
         load_weight("uu", 1)
-        load_child()
-        load_child()
         for a in range(NODE_TILES):
             interleave_x(scopy, a)
         weight_pass("ui", 0, ("wi", 1))
@@ -313,18 +314,23 @@ def tile_childsumtreelstmcell_pb_kernel(
         weight_pass("wu", 1, ("wu", 0))
         load_weight("uo", 1)
         weight_pass("uu", 0, ("wu", 1))
-        weight_pass("uu", 1, ("uu", 0))
-        quantise("uu", 1, 1)
         Q = HALF // 2
-        for l in range(2):
-            interleave_sums(scopy, sum_children(l), l)
+        h_ps = sum_children(0)
+        interleave_sums(scopy, h_ps, 0)
+        h_ps = sum_children(1)
+        interleave_sums(scopy, h_ps, 1)
+        quantise("uu", 0, 1)
         quantise_nodes(h_q, h_grouped, 0, P)
+        regroup(vcopy, "uu", 1, 0, HALF)
+        regroup(scopy, "uu", 1, HALF, HIDDEN)
+        for half in range(2):
+            gate_tile(GATE_I, "wi", "ui", ACT.Sigmoid, half, 0, i_gate)
+        quantise("uu", 1, 0)
         regroup(vcopy, "wo", 0, 0, HALF)
-        gate_tile(GATE_I, "wi", "ui", ACT.Sigmoid, 0, 0, i_gate)
+        quantise("uu", 1, 1)
         regroup(scopy, "wo", 0, HALF, HALF + Q)
         gate_tile(GATE_U, "wu", "uu", ACT.Tanh, 0, 0, u_gate)
         regroup(scopy, "wo", 0, HALF + Q, HIDDEN)
-        gate_tile(GATE_I, "wi", "ui", ACT.Sigmoid, 1, 0, i_gate)
         gate_tile(GATE_U, "wu", "uu", ACT.Tanh, 1, 0, u_gate)
         quantise("wo", 0, 0)
         regroup(vcopy, "wo", 1, 0, HALF)
@@ -371,13 +377,16 @@ def tile_childsumtreelstmcell_pb_kernel(
         flipped = flip_back(u_gate, 1, 1)
         activate(o_acc, GATE_O, ACT.Sigmoid, 0, o_gate)
         cell_state(flipped, 1, 1)
-        quantise("uo", 1, 1)
+        pairs = (range(0, 2), range(2, 4))
+        for pair in pairs:
+            quantise("uo", 1, 1, P * pair[0], P * (pair[-1] + 1))
         o_acc = open_gate("wo", 1)
         mx_pass(o_acc, ("uo", 0, 1), h_q)
-        mx_pass(o_acc, ("uo", 1, 1), h_q, last=True)
-        flipped = [flip_back(o_gate, 0, a) for a in range(NODE_TILES)]
-        activate(o_acc, GATE_O, ACT.Sigmoid, 1, o_gate)
+        for pair in pairs:
+            mx_pass(o_acc, ("uo", 1, 1), h_q, last=True, tiles=pair)
         for a in range(NODE_TILES):
-            hidden_state(flipped[a], 0, a)
-        for a in range(NODE_TILES):
-            hidden_state(flip_back(o_gate, 1, a), 1, a)
+            hidden_state(0, a)
+        for pair in pairs:
+            activate(o_acc, GATE_O, ACT.Sigmoid, 1, o_gate, pair)
+            for a in range(NODE_TILES):
+                hidden_state(1, a, pair)

@@ -341,14 +341,14 @@ def tile_childsumtreelstmcell_pb_kernel(
         flipped.append(flip_back(u_gate, 1, 0))
         h_ps.append(sum_children(3))
         regroup(scopy, "wo", 1, HALF, HALF + Q)
-        interleave_sums(vcopy, h_ps[0], 2)
-        cell_state(flipped[0], 0, 0)
-        quantise("wo", 1, 0)
-        interleave_sums(vcopy, h_ps[1], 3)
-        quantise_nodes(h_q, h_grouped, P, NODES)
+        interleave_sums(scopy, h_ps[0], 2)
         regroup(scopy, "wo", 1, HALF + Q, HIDDEN)
-        cell_state(flipped[1], 1, 0)
         quantise("wo", 0, 1)
+        interleave_sums(scopy, h_ps[1], 3)
+        cell_state(flipped[0], 0, 0)
+        quantise_nodes(h_q, h_grouped, P, NODES)
+        cell_state(flipped[1], 1, 0)
+        quantise("wo", 1, 0)
         V = 352
 
         def share(g, half):

@@ -164,11 +164,11 @@ def tile_childsumtreelstmcell_pb_kernel(
                     stop=last,
                 )
 
-        def open_gate(w, half):
-            acc = [psum.tile([P, NODES], F32, tag="bank", name="acc") for q in range(TILES_PER_HALF)]
+        def open_gate(w, half, tiles=range(TILES_PER_HALF)):
+            opened = {q: psum.tile([P, NODES], F32, tag="bank", name="acc") for q in tiles}
             for g in range(PASSES):
-                mx_pass(acc, (w, g, half), x_q, first=(g == 0))
-            return acc
+                mx_pass(opened, (w, g, half), x_q, first=(g == 0), tiles=tiles)
+            return opened
 
         def activate(acc, m, func, half, result, tiles=range(TILES_PER_HALF)):
             for q in tiles:
@@ -180,7 +180,7 @@ def tile_childsumtreelstmcell_pb_kernel(
                     bias=bias[:, COL_TILES * m + j : COL_TILES * m + j + 1],
                 )
 
-        def gate_tile(m, w, u, func, half, a, result):
+        def products(w, u, half, a):
             acc = psum.tile([P, TILES_PER_HALF, P], F32, tag="bank", name="acc_tile")
             nodes = slice(P * a, P * (a + 1))
             passes = [(label, g, operand) for label, operand in ((w, x_q), (u, h_q)) for g in range(PASSES)]
@@ -196,10 +196,13 @@ def tile_childsumtreelstmcell_pb_kernel(
                         start=(n == 0),
                         stop=(n == len(passes) - 1),
                     )
+            return acc
+
+        def activate_tile(acc, m, func, half, a, result):
             for q in range(TILES_PER_HALF):
                 j = TILES_PER_HALF * half + q
                 nc.scalar.activation(
-                    out=result[:, j, nodes],
+                    out=result[:, j, P * a : P * (a + 1)],
                     in_=acc[:, q, :],
                     func=func,
                     bias=bias[:, COL_TILES * m + j : COL_TILES * m + j + 1],
@@ -227,11 +230,13 @@ def tile_childsumtreelstmcell_pb_kernel(
             nc.vector.tensor_tensor(
                 out=c_sb[:, a, cols], in0=iu_flipped[:], in1=fc_sb[:, a, cols], op=ALU.add
             )
-            nc.scalar.activation(out=tanh_c[:, a, cols], in_=c_sb[:, a, cols], func=ACT.Tanh)
             nc.sync.dma_start(out=out[1, P * a : P * (a + 1), cols], in_=c_sb[:, a, cols])
 
-        def hidden_state(half, a, tiles=range(TILES_PER_HALF)):
-            o_flipped = flip_back(o_gate, half, a, tiles)
+        def tanh_cell(half, a):
+            cols = slice(HALF * half, HALF * (half + 1))
+            nc.scalar.activation(out=tanh_c[:, a, cols], in_=c_sb[:, a, cols], func=ACT.Tanh)
+
+        def hidden_state(o_flipped, half, a, tiles=range(TILES_PER_HALF)):
             cols = slice(HALF * half + P * tiles[0], HALF * half + P * (tiles[-1] + 1))
             nc.vector.tensor_tensor(
                 out=tanh_c[:, a, cols], in0=o_flipped[:], in1=tanh_c[:, a, cols], op=ALU.mult
@@ -273,120 +278,157 @@ def tile_childsumtreelstmcell_pb_kernel(
         tanh_c = keep.tile([P, NODE_TILES, HIDDEN], F32)
         vcopy, scopy = nc.vector.tensor_copy, nc.scalar.copy
 
+        Q = HALF // 2
+        V = 384
+        acc, sums, flips = {}, {}, {}
         load_weight("wi", 0, pieces=4)
         load_weight("wi", 1)
         load_bias()
         nc.sync.dma_start(out=x_sb[:], in_=x.rearrange("(a p) k -> p a k", p=P))
         load_bias()
-        for label, g in (("ui", 0), ("ui", 1), ("wu", 0), ("wu", 1)):
-            load_weight(label, g)
-            load_bias()
-
-        for half in range(2):
-            regroup(vcopy, "wi", 0, HALF * half, HALF * half + HALF // 2)
-            regroup(scopy, "wi", 0, HALF * half + HALF // 2, HALF * (half + 1))
-
-        def weight_pass(label, g, before):
-            regroup(vcopy, label, g, 0, HALF)
-            regroup(scopy, label, g, HALF, HIDDEN)
-            quantise(before[0], before[1], 1)
-            quantise(label, g, 0)
-
+        load_weight("ui", 0)
+        load_bias()
+        load_weight("ui", 1)
+        load_bias()
+        load_weight("wu", 0)
+        load_bias()
+        load_weight("wu", 1)
+        load_bias()
+        regroup(vcopy, "wi", 0, HALF * 0, HALF * 0 + Q)
+        regroup(scopy, "wi", 0, HALF * 0 + Q, HALF * 1)
+        regroup(vcopy, "wi", 0, HALF * 1, HALF * 1 + Q)
+        regroup(scopy, "wi", 0, HALF * 1 + Q, HALF * 2)
         load_weight("uu", 0)
+        load_child()
+        load_child()
         quantise("wi", 0, 0)
-        weight_pass("wi", 1, ("wi", 0))
-        load_child()
-        load_child()
+        regroup(vcopy, "wi", 1, 0, HALF)
+        regroup(scopy, "wi", 1, HALF, HIDDEN)
         load_weight("uu", 1)
-        for a in range(NODE_TILES):
-            interleave_x(scopy, a)
-        weight_pass("ui", 0, ("wi", 1))
+        quantise("wi", 0, 1)
+        quantise("wi", 1, 0)
+        interleave_x(scopy, 0)
+        interleave_x(scopy, 1)
+        regroup(vcopy, "ui", 0, 0, HALF)
+        regroup(scopy, "ui", 0, HALF, HIDDEN)
         load_weight("wo", 0)
+        quantise("wi", 1, 1)
+        quantise("ui", 0, 0)
         quantise_nodes(x_q, x_grouped, 0, NODES)
-        weight_pass("ui", 1, ("ui", 0))
+        regroup(vcopy, "ui", 1, 0, HALF)
+        regroup(scopy, "ui", 1, HALF, HIDDEN)
         load_weight("wo", 1)
         load_child()
         load_child()
         nc.sync.dma_start(out=fc_sb[:], in_=fc_sum.rearrange("(a p) n -> p a n", p=P))
-        weight_pass("wu", 0, ("ui", 1))
+        quantise("ui", 0, 1)
+        quantise("ui", 1, 0)
+        regroup(vcopy, "wu", 0, 0, HALF)
+        regroup(scopy, "wu", 0, HALF, HIDDEN)
         load_weight("uo", 0)
+        quantise("ui", 1, 1)
+        quantise("wu", 0, 0)
         sum_biases()
-        weight_pass("wu", 1, ("wu", 0))
+        regroup(vcopy, "wu", 1, 0, HALF)
+        regroup(scopy, "wu", 1, HALF, HIDDEN)
         load_weight("uo", 1)
-        weight_pass("uu", 0, ("wu", 1))
-        Q = HALF // 2
-        h_ps = sum_children(0)
-        interleave_sums(scopy, h_ps, 0)
-        h_ps = sum_children(1)
-        interleave_sums(scopy, h_ps, 1)
+        quantise("wu", 0, 1)
+        quantise("wu", 1, 0)
+        regroup(vcopy, "uu", 0, 0, HALF)
+        regroup(scopy, "uu", 0, HALF, HIDDEN)
+        quantise("wu", 1, 1)
+        quantise("uu", 0, 0)
+        sums[0] = sum_children(0)
+        interleave_sums(scopy, sums[0], 0)
+        sums[1] = sum_children(1)
+        interleave_sums(scopy, sums[1], 1)
         quantise("uu", 0, 1)
-        quantise_nodes(h_q, h_grouped, 0, P)
+        quantise_nodes(h_q, h_grouped, P * 0, P * 1)
         regroup(vcopy, "uu", 1, 0, HALF)
         regroup(scopy, "uu", 1, HALF, HIDDEN)
-        for half in range(2):
-            gate_tile(GATE_I, "wi", "ui", ACT.Sigmoid, half, 0, i_gate)
+        acc["i", 0, 0] = products("wi", "ui", 0, 0)
+        activate_tile(acc["i", 0, 0], GATE_I, ACT.Sigmoid, 0, 0, i_gate)
+        acc["i", 1, 0] = products("wi", "ui", 1, 0)
+        activate_tile(acc["i", 1, 0], GATE_I, ACT.Sigmoid, 1, 0, i_gate)
         quantise("uu", 1, 0)
         regroup(vcopy, "wo", 0, 0, HALF)
         quantise("uu", 1, 1)
         regroup(scopy, "wo", 0, HALF, HALF + Q)
-        gate_tile(GATE_U, "wu", "uu", ACT.Tanh, 0, 0, u_gate)
+        acc["u", 0, 0] = products("wu", "uu", 0, 0)
+        activate_tile(acc["u", 0, 0], GATE_U, ACT.Tanh, 0, 0, u_gate)
         regroup(scopy, "wo", 0, HALF + Q, HIDDEN)
-        gate_tile(GATE_U, "wu", "uu", ACT.Tanh, 1, 0, u_gate)
+        acc["u", 1, 0] = products("wu", "uu", 1, 0)
+        activate_tile(acc["u", 1, 0], GATE_U, ACT.Tanh, 1, 0, u_gate)
         quantise("wo", 0, 0)
         regroup(vcopy, "wo", 1, 0, HALF)
         multiply_gates(0, 0)
-        h_ps = [sum_children(2)]
-        flipped = [flip_back(u_gate, 0, 0)]
+        quantise("wo", 1, 0)
+        sums[2] = sum_children(2)
+        flips[0, 0] = flip_back(u_gate, 0, 0)
         multiply_gates(1, 0)
-        flipped.append(flip_back(u_gate, 1, 0))
-        h_ps.append(sum_children(3))
+        flips[1, 0] = flip_back(u_gate, 1, 0)
+        sums[3] = sum_children(3)
+        acc["o", 0] = open_gate("wo", 0)
         regroup(scopy, "wo", 1, HALF, HALF + Q)
-        interleave_sums(scopy, h_ps[0], 2)
+        interleave_sums(scopy, sums[2], 2)
         regroup(scopy, "wo", 1, HALF + Q, HIDDEN)
         quantise("wo", 0, 1)
-        interleave_sums(scopy, h_ps[1], 3)
-        cell_state(flipped[0], 0, 0)
-        quantise_nodes(h_q, h_grouped, P, NODES)
-        cell_state(flipped[1], 1, 0)
-        quantise("wo", 1, 0)
-        V = 352
-
-        def share(g, half):
-            regroup(vcopy, "uo", g, HALF * half, HALF * half + V)
-            regroup(scopy, "uo", g, HALF * half + V, HALF * (half + 1))
-
-        share(0, 0)
+        interleave_sums(scopy, sums[3], 3)
+        cell_state(flips[0, 0], 0, 0)
+        quantise_nodes(h_q, h_grouped, P * 1, P * 2)
+        cell_state(flips[1, 0], 1, 0)
+        regroup(scopy, "uo", 0, HALF * 0 + V, HALF * 1)
+        regroup(scopy, "uo", 0, HALF * 1 + V, HALF * 2)
+        regroup(vcopy, "uo", 0, HALF * 0, HALF * 0 + V)
+        acc["i", 0, 1] = products("wi", "ui", 0, 1)
+        tanh_cell(0, 0)
+        activate_tile(acc["i", 0, 1], GATE_I, ACT.Sigmoid, 0, 1, i_gate)
+        acc["u", 0, 1] = products("wu", "uu", 0, 1)
+        regroup(vcopy, "uo", 0, HALF * 1, HALF * 1 + V)
         quantise("wo", 1, 1)
-        share(0, 1)
-        gate_tile(GATE_I, "wi", "ui", ACT.Sigmoid, 0, 1, i_gate)
-        gate_tile(GATE_U, "wu", "uu", ACT.Tanh, 0, 1, u_gate)
+        activate_tile(acc["u", 0, 1], GATE_U, ACT.Tanh, 0, 1, u_gate)
         quantise("uo", 0, 0)
+        acc["i", 1, 1] = products("wi", "ui", 1, 1)
+        acc["u", 1, 1] = products("wu", "uu", 1, 1)
         multiply_gates(0, 1)
+        flips[0, 1] = flip_back(u_gate, 0, 1)
         quantise("uo", 0, 1)
-        share(1, 0)
-        gate_tile(GATE_I, "wi", "ui", ACT.Sigmoid, 1, 1, i_gate)
-        gate_tile(GATE_U, "wu", "uu", ACT.Tanh, 1, 1, u_gate)
-        flipped = flip_back(u_gate, 0, 1)
-        cell_state(flipped, 0, 1)
+        regroup(scopy, "uo", 1, HALF * 0 + V, HALF * 1)
+        regroup(vcopy, "uo", 1, HALF * 0, HALF * 0 + V)
+        tanh_cell(1, 0)
+        activate_tile(acc["i", 1, 1], GATE_I, ACT.Sigmoid, 1, 1, i_gate)
+        cell_state(flips[0, 1], 0, 1)
+        activate_tile(acc["u", 1, 1], GATE_U, ACT.Tanh, 1, 1, u_gate)
         quantise("uo", 1, 0)
         multiply_gates(1, 1)
-        share(1, 1)
-        o_acc = open_gate("wo", 0)
-        mx_pass(o_acc, ("uo", 0, 0), h_q)
-        mx_pass(o_acc, ("uo", 1, 0), h_q, last=True)
-        flipped = flip_back(u_gate, 1, 1)
-        activate(o_acc, GATE_O, ACT.Sigmoid, 0, o_gate)
-        cell_state(flipped, 1, 1)
-        pairs = (range(0, 2), range(2, 4))
-        for pair in pairs:
-            quantise("uo", 1, 1, P * pair[0], P * (pair[-1] + 1))
-        o_acc = open_gate("wo", 1)
-        mx_pass(o_acc, ("uo", 0, 1), h_q)
-        for pair in pairs:
-            mx_pass(o_acc, ("uo", 1, 1), h_q, last=True, tiles=pair)
-        for a in range(NODE_TILES):
-            hidden_state(0, a)
-        for pair in pairs:
-            activate(o_acc, GATE_O, ACT.Sigmoid, 1, o_gate, pair)
-            for a in range(NODE_TILES):
-                hidden_state(1, a, pair)
+        regroup(scopy, "uo", 1, HALF * 1 + V, HALF * 2)
+        tanh_cell(0, 1)
+        mx_pass(acc["o", 0], ("uo", 0, 0), h_q)
+        regroup(vcopy, "uo", 1, HALF * 1, HALF * 1 + V)
+        acc["o", 1] = open_gate("wo", 1, range(0, 2))
+        mx_pass(acc["o", 1], ("uo", 0, 1), h_q, tiles=range(0, 2))
+        mx_pass(acc["o", 0], ("uo", 1, 0), h_q, last=True)
+        flips[1, 1] = flip_back(u_gate, 1, 1)
+        activate(acc["o", 0], GATE_O, ACT.Sigmoid, 0, o_gate)
+        quantise("uo", 1, 1, P * 0, P * 2)
+        cell_state(flips[1, 1], 1, 1)
+        quantise("uo", 1, 1, P * 2, P * 4)
+        acc["o", 1].update(open_gate("wo", 1, range(2, 4)))
+        mx_pass(acc["o", 1], ("uo", 0, 1), h_q, tiles=range(2, 4))
+        flips["o", 0, 0] = flip_back(o_gate, 0, 0)
+        flips["o", 0, 1] = flip_back(o_gate, 0, 1)
+        hidden_state(flips["o", 0, 0], 0, 0)
+        tanh_cell(1, 1)
+        hidden_state(flips["o", 0, 1], 0, 1)
+        mx_pass(acc["o", 1], ("uo", 1, 1), h_q, last=True, tiles=range(0, 2))
+        mx_pass(acc["o", 1], ("uo", 1, 1), h_q, last=True, tiles=range(2, 4))
+        activate(acc["o", 1], GATE_O, ACT.Sigmoid, 1, o_gate, range(0, 2))
+        flips["o", 1, 0] = flip_back(o_gate, 1, 0, range(0, 2))
+        hidden_state(flips["o", 1, 0], 1, 0, range(0, 2))
+        flips["o", 1, 1] = flip_back(o_gate, 1, 1, range(0, 2))
+        hidden_state(flips["o", 1, 1], 1, 1, range(0, 2))
+        activate(acc["o", 1], GATE_O, ACT.Sigmoid, 1, o_gate, range(2, 4))
+        flips["o", 1, 0] = flip_back(o_gate, 1, 0, range(2, 4))
+        hidden_state(flips["o", 1, 0], 1, 0, range(2, 4))
+        flips["o", 1, 1] = flip_back(o_gate, 1, 1, range(2, 4))
+        hidden_state(flips["o", 1, 1], 1, 1, range(2, 4))

@@ -375,17 +375,17 @@ def tile_childsumtreelstmcell_pb_kernel(
         quantise("wo", 0, 1)
         interleave_sums(scopy, sums[3], 3)
         cell_state(flips[0, 0], 0, 0)
+        tanh_cell(0, 0)
+        quantise("wo", 1, 1)
         quantise_nodes(h_q, h_grouped, P * 1, P * 2)
         cell_state(flips[1, 0], 1, 0)
         regroup(scopy, "uo", 0, HALF * 0 + V, HALF * 1)
         regroup(scopy, "uo", 0, HALF * 1 + V, HALF * 2)
         regroup(vcopy, "uo", 0, HALF * 0, HALF * 0 + V)
         acc["i", 0, 1] = products("wi", "ui", 0, 1)
-        tanh_cell(0, 0)
         activate_tile(acc["i", 0, 1], GATE_I, ACT.Sigmoid, 0, 1, i_gate)
         acc["u", 0, 1] = products("wu", "uu", 0, 1)
         regroup(vcopy, "uo", 0, HALF * 1, HALF * 1 + V)
-        quantise("wo", 1, 1)
         activate_tile(acc["u", 0, 1], GATE_U, ACT.Tanh, 0, 1, u_gate)
         quantise("uo", 0, 0)
         acc["i", 1, 1] = products("wi", "ui", 1, 1)

@@ -118,31 +118,30 @@ def tile_childsumtreelstmcell_pb_kernel(
             nc.sync.dma_start(out=child[:], in_=child_rows[len(children)])
             children.append(child)
 
-        def sum_children(l):
+        def sum_children(l, g):
             by_word = children[l][:].rearrange("q s (g p t) -> q s g t p", g=PASSES, t=PACK)
-            h_ps = psum.tile([P, PASSES, PACK, NODES_PER_LOAD], F32, tag="bank", name="h_ps")
-            for g in range(PASSES):
-                for t in range(PACK):
-                    for s in range(ROWS_PER_PARTITION):
-                        nc.tensor.matmul(
-                            out=h_ps[:, g, t, :],
-                            lhsT=by_word[:, s, g, t, :],
-                            rhs=pair_sum[:],
-                            start=(s == 0),
-                            stop=(s == ROWS_PER_PARTITION - 1),
-                        )
+            h_ps = psum.tile([P, PACK, NODES_PER_LOAD], F32, tag="bank", name="h_ps")
+            for t in range(PACK):
+                for s in range(ROWS_PER_PARTITION):
+                    nc.tensor.matmul(
+                        out=h_ps[:, t, :],
+                        lhsT=by_word[:, s, g, t, :],
+                        rhs=pair_sum[:],
+                        start=(s == 0),
+                        stop=(s == ROWS_PER_PARTITION - 1),
+                    )
             return h_ps
 
-        def interleave_sums(copy, h_ps, l):
+        def interleave_sums(copy, h_ps, l, g):
             first = NODES_PER_LOAD * l
             copy(
-                out=h_grouped[:, :, first : first + NODES_PER_LOAD, :],
-                in_=h_ps[:].rearrange("p g t n -> p g n t"),
+                out=h_grouped[:, g, first : first + NODES_PER_LOAD, :],
+                in_=h_ps[:].rearrange("p t n -> p n t"),
             )
 
-        def quantise_nodes(operand, grouped, first, end):
+        def quantise_nodes(operand, grouped, first, end, passes=range(PASSES)):
             node_words, node_scales = operand
-            for g in range(PASSES):
+            for g in passes:
                 nc.vector.quantize_mx(
                     out=node_words[:, g, first:end].bitcast(FP8X4),
                     scales=node_scales[:, g, first:end],
@@ -338,10 +337,14 @@ def tile_childsumtreelstmcell_pb_kernel(
         regroup(scopy, "uu", 0, HALF, HIDDEN)
         quantise("wu", 1, 1)
         quantise("uu", 0, 0)
-        sums[0] = sum_children(0)
-        interleave_sums(scopy, sums[0], 0)
-        sums[1] = sum_children(1)
-        interleave_sums(scopy, sums[1], 1)
+        sums[0, 0] = sum_children(0, 0)
+        sums[0, 1] = sum_children(0, 1)
+        interleave_sums(scopy, sums[0, 0], 0, 0)
+        interleave_sums(scopy, sums[0, 1], 0, 1)
+        sums[1, 0] = sum_children(1, 0)
+        sums[1, 1] = sum_children(1, 1)
+        interleave_sums(scopy, sums[1, 0], 1, 0)
+        interleave_sums(scopy, sums[1, 1], 1, 1)
         quantise("uu", 0, 1)
         quantise_nodes(h_q, h_grouped, P * 0, P * 1)
         regroup(vcopy, "uu", 1, 0, HALF)
@@ -363,21 +366,25 @@ def tile_childsumtreelstmcell_pb_kernel(
         regroup(vcopy, "wo", 1, 0, HALF)
         multiply_gates(0, 0)
         quantise("wo", 1, 0)
-        sums[2] = sum_children(2)
+        sums[2, 0] = sum_children(2, 0)
+        sums[2, 1] = sum_children(2, 1)
         flips[0, 0] = flip_back(u_gate, 0, 0)
         multiply_gates(1, 0)
         flips[1, 0] = flip_back(u_gate, 1, 0)
-        sums[3] = sum_children(3)
-        acc["o", 0] = open_gate("wo", 0)
         regroup(scopy, "wo", 1, HALF, HALF + Q)
-        interleave_sums(scopy, sums[2], 2)
+        interleave_sums(scopy, sums[2, 0], 2, 0)
+        interleave_sums(scopy, sums[2, 1], 2, 1)
+        sums[3, 0] = sum_children(3, 0)
+        sums[3, 1] = sum_children(3, 1)
+        acc["o", 0] = open_gate("wo", 0)
         regroup(scopy, "wo", 1, HALF + Q, HIDDEN)
         quantise("wo", 0, 1)
-        interleave_sums(scopy, sums[3], 3)
+        interleave_sums(scopy, sums[3, 0], 3, 0)
+        interleave_sums(scopy, sums[3, 1], 3, 1)
         cell_state(flips[0, 0], 0, 0)
         tanh_cell(0, 0)
-        quantise("wo", 1, 1)
         quantise_nodes(h_q, h_grouped, P * 1, P * 2)
+        quantise("wo", 1, 1)
         cell_state(flips[1, 0], 1, 0)
         regroup(scopy, "uo", 0, HALF * 0 + V, HALF * 1)
         regroup(scopy, "uo", 0, HALF * 1 + V, HALF * 2)

@@ -25,9 +25,11 @@ BANK = 512
 HALF = HIDDEN // 2
 TILES_PER_HALF = HALF // P
 
-ROWS_PER_PARTITION = 4
-PAIR = CHILDREN // ROWS_PER_PARTITION
-NODES_PER_LOAD = P // PAIR
+ROWS = 2
+QUAD = CHILDREN // ROWS
+NODES_PER_SUM = P // QUAD
+SUMS_PER_LOAD = 2
+NODES_PER_LOAD = SUMS_PER_LOAD * NODES_PER_SUM
 
 GATE_I, GATE_U, GATE_O = 0, 1, 2
 
@@ -49,12 +51,12 @@ def tile_childsumtreelstmcell_pb_kernel(
 
         ident = const.tile([P, P], F32)
         make_identity(nc, ident[:])
-        pair_sum_f32 = const.tile([P, P // PAIR], F32)
+        quad_sum_f32 = const.tile([P, NODES_PER_SUM], F32)
         nc.vector.reduce_sum(
-            out=pair_sum_f32[:], in_=ident[:].rearrange("q (i r) -> q i r", r=PAIR), axis=mybir.AxisListType.X
+            out=quad_sum_f32[:], in_=ident[:].rearrange("q (i r) -> q i r", r=QUAD), axis=mybir.AxisListType.X
         )
-        pair_sum = const.tile([P, P // PAIR], BF16)
-        nc.vector.tensor_copy(out=pair_sum[:], in_=pair_sum_f32[:])
+        quad_sum = const.tile([P, NODES_PER_SUM], BF16)
+        nc.vector.tensor_copy(out=quad_sum[:], in_=quad_sum_f32[:])
 
         zero_col = const.tile([P, 1], F32)
         nc.vector.memset(zero_col[:], 0.0)
@@ -63,21 +65,21 @@ def tile_childsumtreelstmcell_pb_kernel(
 
         bias_rows = const.tile([P, P], BF16)
         nc.vector.memset(bias_rows[:], 0.0)
-        bias = const.tile([P, P // PAIR], F32)
+        bias = const.tile([P, NODES_PER_SUM], F32)
 
         bias_vectors = [(m, r, b) for m, pair in enumerate(((bWi, bUi), (bWu, bUu), (bWo, bUo))) for r, b in enumerate(pair)]
 
         def load_bias():
             m, r, b = bias_vectors.pop()
-            first = PAIR * COL_TILES * m + r
+            first = QUAD * COL_TILES * m + r
             nc.sync.dma_start(
-                out=bias_rows[first : PAIR * COL_TILES * (m + 1) : PAIR, :],
+                out=bias_rows[first : QUAD * COL_TILES * (m + 1) : QUAD, :],
                 in_=b.rearrange("(j p) -> j p", p=P),
             )
 
         def sum_biases():
-            bias_ps = psum.tile([P, P // PAIR], F32, tag="bank")
-            nc.tensor.matmul(out=bias_ps[:], lhsT=bias_rows[:], rhs=pair_sum[:], start=True, stop=True)
+            bias_ps = psum.tile([P, NODES_PER_SUM], F32, tag="bank")
+            nc.tensor.matmul(out=bias_ps[:], lhsT=bias_rows[:], rhs=quad_sum[:], start=True, stop=True)
             nc.vector.tensor_copy(out=bias[:], in_=bias_ps[:])
 
         weights = {"wi": Wi, "ui": Ui, "wu": Wu, "uu": Uu, "wo": Wo, "uo": Uo}
@@ -93,6 +95,9 @@ def tile_childsumtreelstmcell_pb_kernel(
             raws[label, g] = raw
             words[label, g] = keep.tile([P, HIDDEN], U32, align_bytes=64, name="words_%s%d" % (label, g))
             scales[label, g] = keep.tile([P, HIDDEN], U8, align_bytes=64, name="scales_%s%d" % (label, g))
+
+        def load_fc(a):
+            nc.sync.dma_start(out=fc_sb[:, a, :], in_=fc_sum[P * a : P * (a + 1), :])
 
         def regroup(copy, label, g, first, end):
             half = first // HALF
@@ -114,22 +119,23 @@ def tile_childsumtreelstmcell_pb_kernel(
             )
 
         def load_child():
-            child = child_pool.tile([P, ROWS_PER_PARTITION, FEATURES], BF16, name="child")
+            child = child_pool.tile([P, SUMS_PER_LOAD, ROWS, FEATURES], BF16, name="child")
             nc.sync.dma_start(out=child[:], in_=child_rows[len(children)])
             children.append(child)
 
         def sum_children(l, g):
-            by_word = children[l][:].rearrange("q s (g p t) -> q s g t p", g=PASSES, t=PACK)
+            by_word = children[l][:].rearrange("q j s (g p t) -> q j s g t p", g=PASSES, t=PACK)
             h_ps = psum.tile([P, PACK, NODES_PER_LOAD], F32, tag="bank", name="h_ps")
             for t in range(PACK):
-                for s in range(ROWS_PER_PARTITION):
-                    nc.tensor.matmul(
-                        out=h_ps[:, t, :],
-                        lhsT=by_word[:, s, g, t, :],
-                        rhs=pair_sum[:],
-                        start=(s == 0),
-                        stop=(s == ROWS_PER_PARTITION - 1),
-                    )
+                for j in range(SUMS_PER_LOAD):
+                    for s in range(ROWS):
+                        nc.tensor.matmul(
+                            out=h_ps[:, t, NODES_PER_SUM * j : NODES_PER_SUM * (j + 1)],
+                            lhsT=by_word[:, j, s, g, t, :],
+                            rhs=quad_sum[:],
+                            start=(s == 0),
+                            stop=(s == ROWS - 1),
+                        )
             return h_ps
 
         def interleave_sums(copy, h_ps, l, g):
@@ -256,7 +262,7 @@ def tile_childsumtreelstmcell_pb_kernel(
             )
 
         child_rows = child_h.rearrange("n c k -> (n c) k").rearrange(
-            "(l q s) k -> l q s k", q=P, s=ROWS_PER_PARTITION
+            "(l j q s) k -> l q j s k", j=SUMS_PER_LOAD, q=P, s=ROWS
         )
         children = []
         node_operands = []
@@ -319,7 +325,7 @@ def tile_childsumtreelstmcell_pb_kernel(
         load_weight("wo", 1)
         load_child()
         load_child()
-        nc.sync.dma_start(out=fc_sb[:], in_=fc_sum.rearrange("(a p) n -> p a n", p=P))
+        load_fc(0)
         quantise("ui", 0, 1)
         quantise("ui", 1, 0)
         regroup(vcopy, "wu", 0, 0, HALF)
@@ -331,6 +337,7 @@ def tile_childsumtreelstmcell_pb_kernel(
         regroup(vcopy, "wu", 1, 0, HALF)
         regroup(scopy, "wu", 1, HALF, HIDDEN)
         load_weight("uo", 1)
+        load_fc(1)
         quantise("wu", 0, 1)
         quantise("wu", 1, 0)
         regroup(vcopy, "uu", 0, 0, HALF)
@@ -348,15 +355,17 @@ def tile_childsumtreelstmcell_pb_kernel(
         quantise("uu", 0, 1)
         quantise_nodes(h_q, h_grouped, P * 0, P * 1)
         regroup(vcopy, "uu", 1, 0, HALF)
-        regroup(scopy, "uu", 1, HALF, HIDDEN)
+        regroup(vcopy, "uu", 1, HALF, HALF + P)
+        regroup(scopy, "uu", 1, HALF + P, HIDDEN)
         acc["i", 0, 0] = products("wi", "ui", 0, 0)
         activate_tile(acc["i", 0, 0], GATE_I, ACT.Sigmoid, 0, 0, i_gate)
         acc["i", 1, 0] = products("wi", "ui", 1, 0)
         activate_tile(acc["i", 1, 0], GATE_I, ACT.Sigmoid, 1, 0, i_gate)
         quantise("uu", 1, 0)
         regroup(vcopy, "wo", 0, 0, HALF)
+        regroup(vcopy, "wo", 0, HALF, HALF + P)
         quantise("uu", 1, 1)
-        regroup(scopy, "wo", 0, HALF, HALF + Q)
+        regroup(scopy, "wo", 0, HALF + P, HALF + Q)
         acc["u", 0, 0] = products("wu", "uu", 0, 0)
         activate_tile(acc["u", 0, 0], GATE_U, ACT.Tanh, 0, 0, u_gate)
         regroup(scopy, "wo", 0, HALF + Q, HIDDEN)
@@ -364,6 +373,7 @@ def tile_childsumtreelstmcell_pb_kernel(
         activate_tile(acc["u", 1, 0], GATE_U, ACT.Tanh, 1, 0, u_gate)
         quantise("wo", 0, 0)
         regroup(vcopy, "wo", 1, 0, HALF)
+        regroup(vcopy, "wo", 1, HALF, HALF + P)
         multiply_gates(0, 0)
         quantise("wo", 1, 0)
         sums[2, 0] = sum_children(2, 0)
@@ -371,20 +381,20 @@ def tile_childsumtreelstmcell_pb_kernel(
         flips[0, 0] = flip_back(u_gate, 0, 0)
         multiply_gates(1, 0)
         flips[1, 0] = flip_back(u_gate, 1, 0)
-        regroup(scopy, "wo", 1, HALF, HALF + Q)
+        regroup(scopy, "wo", 1, HALF + P, HALF + Q)
+        regroup(scopy, "wo", 1, HALF + Q, HIDDEN)
         interleave_sums(scopy, sums[2, 0], 2, 0)
         interleave_sums(scopy, sums[2, 1], 2, 1)
         sums[3, 0] = sum_children(3, 0)
         sums[3, 1] = sum_children(3, 1)
         acc["o", 0] = open_gate("wo", 0)
-        regroup(scopy, "wo", 1, HALF + Q, HIDDEN)
         quantise("wo", 0, 1)
         interleave_sums(scopy, sums[3, 0], 3, 0)
         interleave_sums(scopy, sums[3, 1], 3, 1)
+        quantise("wo", 1, 1)
         cell_state(flips[0, 0], 0, 0)
         tanh_cell(0, 0)
         quantise_nodes(h_q, h_grouped, P * 1, P * 2)
-        quantise("wo", 1, 1)
         cell_state(flips[1, 0], 1, 0)
         regroup(scopy, "uo", 0, HALF * 0 + V, HALF * 1)
         regroup(scopy, "uo", 0, HALF * 1 + V, HALF * 2)
@@ -395,46 +405,46 @@ def tile_childsumtreelstmcell_pb_kernel(
         regroup(vcopy, "uo", 0, HALF * 1, HALF * 1 + V)
         activate_tile(acc["u", 0, 1], GATE_U, ACT.Tanh, 0, 1, u_gate)
         quantise("uo", 0, 0)
-        acc["i", 1, 1] = products("wi", "ui", 1, 1)
         acc["u", 1, 1] = products("wu", "uu", 1, 1)
-        multiply_gates(0, 1)
-        flips[0, 1] = flip_back(u_gate, 0, 1)
-        quantise("uo", 0, 1)
+        acc["i", 1, 1] = products("wi", "ui", 1, 1)
         regroup(scopy, "uo", 1, HALF * 0 + V, HALF * 1)
         regroup(vcopy, "uo", 1, HALF * 0, HALF * 0 + V)
         tanh_cell(1, 0)
-        activate_tile(acc["i", 1, 1], GATE_I, ACT.Sigmoid, 1, 1, i_gate)
-        cell_state(flips[0, 1], 0, 1)
+        multiply_gates(0, 1)
         activate_tile(acc["u", 1, 1], GATE_U, ACT.Tanh, 1, 1, u_gate)
+        activate_tile(acc["i", 1, 1], GATE_I, ACT.Sigmoid, 1, 1, i_gate)
         quantise("uo", 1, 0)
-        multiply_gates(1, 1)
-        regroup(scopy, "uo", 1, HALF * 1 + V, HALF * 2)
-        tanh_cell(0, 1)
         mx_pass(acc["o", 0], ("uo", 0, 0), h_q)
-        regroup(vcopy, "uo", 1, HALF * 1, HALF * 1 + V)
-        acc["o", 1] = open_gate("wo", 1, range(0, 2))
-        mx_pass(acc["o", 1], ("uo", 0, 1), h_q, tiles=range(0, 2))
         mx_pass(acc["o", 0], ("uo", 1, 0), h_q, last=True)
-        flips[1, 1] = flip_back(u_gate, 1, 1)
+        acc["o", 1] = open_gate("wo", 1, range(0, 2))
+        quantise("uo", 0, 1)
+        mx_pass(acc["o", 1], ("uo", 0, 1), h_q, tiles=range(0, 2))
+        flips[0, 1] = flip_back(u_gate, 0, 1)
         activate(acc["o", 0], GATE_O, ACT.Sigmoid, 0, o_gate)
+        regroup(scopy, "uo", 1, HALF * 1 + V, HALF * 2)
+        regroup(vcopy, "uo", 1, HALF * 1, HALF * 1 + V)
+        multiply_gates(1, 1)
         quantise("uo", 1, 1, P * 0, P * 2)
-        cell_state(flips[1, 1], 1, 1)
-        quantise("uo", 1, 1, P * 2, P * 4)
+        flips["o", 0, 0] = flip_back(o_gate, 0, 0)
+        flips[1, 1] = flip_back(u_gate, 1, 1)
+        cell_state(flips[0, 1], 0, 1)
+        tanh_cell(0, 1)
+        flips["o", 0, 1] = flip_back(o_gate, 0, 1)
+        mx_pass(acc["o", 1], ("uo", 1, 1), h_q, last=True, tiles=range(0, 2))
+        activate(acc["o", 1], GATE_O, ACT.Sigmoid, 1, o_gate, range(0, 2))
         acc["o", 1].update(open_gate("wo", 1, range(2, 4)))
         mx_pass(acc["o", 1], ("uo", 0, 1), h_q, tiles=range(2, 4))
-        flips["o", 0, 0] = flip_back(o_gate, 0, 0)
-        flips["o", 0, 1] = flip_back(o_gate, 0, 1)
-        hidden_state(flips["o", 0, 0], 0, 0)
-        tanh_cell(1, 1)
-        hidden_state(flips["o", 0, 1], 0, 1)
-        mx_pass(acc["o", 1], ("uo", 1, 1), h_q, last=True, tiles=range(0, 2))
+        quantise("uo", 1, 1, P * 2, P * 4)
+        cell_state(flips[1, 1], 1, 1)
         mx_pass(acc["o", 1], ("uo", 1, 1), h_q, last=True, tiles=range(2, 4))
-        activate(acc["o", 1], GATE_O, ACT.Sigmoid, 1, o_gate, range(0, 2))
+        tanh_cell(1, 1)
+        hidden_state(flips["o", 0, 0], 0, 0)
+        hidden_state(flips["o", 0, 1], 0, 1)
         flips["o", 1, 0] = flip_back(o_gate, 1, 0, range(0, 2))
-        hidden_state(flips["o", 1, 0], 1, 0, range(0, 2))
         flips["o", 1, 1] = flip_back(o_gate, 1, 1, range(0, 2))
-        hidden_state(flips["o", 1, 1], 1, 1, range(0, 2))
         activate(acc["o", 1], GATE_O, ACT.Sigmoid, 1, o_gate, range(2, 4))
+        hidden_state(flips["o", 1, 0], 1, 0, range(0, 2))
+        hidden_state(flips["o", 1, 1], 1, 1, range(0, 2))
         flips["o", 1, 0] = flip_back(o_gate, 1, 0, range(2, 4))
         hidden_state(flips["o", 1, 0], 1, 0, range(2, 4))
         flips["o", 1, 1] = flip_back(o_gate, 1, 1, range(2, 4))

@@ -25,11 +25,9 @@ BANK = 512
 HALF = HIDDEN // 2
 TILES_PER_HALF = HALF // P
 
-ROWS = 2
-QUAD = CHILDREN // ROWS
-NODES_PER_SUM = P // QUAD
-SUMS_PER_LOAD = 2
-NODES_PER_LOAD = SUMS_PER_LOAD * NODES_PER_SUM
+ROWS_PER_PARTITION = 4
+PAIR = CHILDREN // ROWS_PER_PARTITION
+NODES_PER_LOAD = P // PAIR
 
 GATE_I, GATE_U, GATE_O = 0, 1, 2
 
@@ -51,12 +49,12 @@ def tile_childsumtreelstmcell_pb_kernel(
 
         ident = const.tile([P, P], F32)
         make_identity(nc, ident[:])
-        quad_sum_f32 = const.tile([P, NODES_PER_SUM], F32)
+        pair_sum_f32 = const.tile([P, P // PAIR], F32)
         nc.vector.reduce_sum(
-            out=quad_sum_f32[:], in_=ident[:].rearrange("q (i r) -> q i r", r=QUAD), axis=mybir.AxisListType.X
+            out=pair_sum_f32[:], in_=ident[:].rearrange("q (i r) -> q i r", r=PAIR), axis=mybir.AxisListType.X
         )
-        quad_sum = const.tile([P, NODES_PER_SUM], BF16)
-        nc.vector.tensor_copy(out=quad_sum[:], in_=quad_sum_f32[:])
+        pair_sum = const.tile([P, P // PAIR], BF16)
+        nc.vector.tensor_copy(out=pair_sum[:], in_=pair_sum_f32[:])
 
         zero_col = const.tile([P, 1], F32)
         nc.vector.memset(zero_col[:], 0.0)
@@ -65,21 +63,21 @@ def tile_childsumtreelstmcell_pb_kernel(
 
         bias_rows = const.tile([P, P], BF16)
         nc.vector.memset(bias_rows[:], 0.0)
-        bias = const.tile([P, NODES_PER_SUM], F32)
+        bias = const.tile([P, P // PAIR], F32)
 
         bias_vectors = [(m, r, b) for m, pair in enumerate(((bWi, bUi), (bWu, bUu), (bWo, bUo))) for r, b in enumerate(pair)]
 
         def load_bias():
             m, r, b = bias_vectors.pop()
-            first = QUAD * COL_TILES * m + r
+            first = PAIR * COL_TILES * m + r
             nc.sync.dma_start(
-                out=bias_rows[first : QUAD * COL_TILES * (m + 1) : QUAD, :],
+                out=bias_rows[first : PAIR * COL_TILES * (m + 1) : PAIR, :],
                 in_=b.rearrange("(j p) -> j p", p=P),
             )
 
         def sum_biases():
-            bias_ps = psum.tile([P, NODES_PER_SUM], F32, tag="bank")
-            nc.tensor.matmul(out=bias_ps[:], lhsT=bias_rows[:], rhs=quad_sum[:], start=True, stop=True)
+            bias_ps = psum.tile([P, P // PAIR], F32, tag="bank")
+            nc.tensor.matmul(out=bias_ps[:], lhsT=bias_rows[:], rhs=pair_sum[:], start=True, stop=True)
             nc.vector.tensor_copy(out=bias[:], in_=bias_ps[:])
 
         weights = {"wi": Wi, "ui": Ui, "wu": Wu, "uu": Uu, "wo": Wo, "uo": Uo}
@@ -119,23 +117,22 @@ def tile_childsumtreelstmcell_pb_kernel(
             )
 
         def load_child():
-            child = child_pool.tile([P, SUMS_PER_LOAD, ROWS, FEATURES], BF16, name="child")
+            child = child_pool.tile([P, ROWS_PER_PARTITION, FEATURES], BF16, name="child")
             nc.sync.dma_start(out=child[:], in_=child_rows[len(children)])
             children.append(child)
 
         def sum_children(l, g):
-            by_word = children[l][:].rearrange("q j s (g p t) -> q j s g t p", g=PASSES, t=PACK)
+            by_word = children[l][:].rearrange("q s (g p t) -> q s g t p", g=PASSES, t=PACK)
             h_ps = psum.tile([P, PACK, NODES_PER_LOAD], F32, tag="bank", name="h_ps")
             for t in range(PACK):
-                for j in range(SUMS_PER_LOAD):
-                    for s in range(ROWS):
-                        nc.tensor.matmul(
-                            out=h_ps[:, t, NODES_PER_SUM * j : NODES_PER_SUM * (j + 1)],
-                            lhsT=by_word[:, j, s, g, t, :],
-                            rhs=quad_sum[:],
-                            start=(s == 0),
-                            stop=(s == ROWS - 1),
-                        )
+                for s in range(ROWS_PER_PARTITION):
+                    nc.tensor.matmul(
+                        out=h_ps[:, t, :],
+                        lhsT=by_word[:, s, g, t, :],
+                        rhs=pair_sum[:],
+                        start=(s == 0),
+                        stop=(s == ROWS_PER_PARTITION - 1),
+                    )
             return h_ps
 
         def interleave_sums(copy, h_ps, l, g):
@@ -262,7 +259,7 @@ def tile_childsumtreelstmcell_pb_kernel(
             )
 
         child_rows = child_h.rearrange("n c k -> (n c) k").rearrange(
-            "(l j q s) k -> l q j s k", j=SUMS_PER_LOAD, q=P, s=ROWS
+            "(l q s) k -> l q s k", q=P, s=ROWS_PER_PARTITION
         )
         children = []
         node_operands = []

@@ -24,6 +24,7 @@ COL_TILES = HIDDEN // P
 BANK = 512
 HALF = HIDDEN // 2
 TILES_PER_HALF = HALF // P
+EXTRA = 64
 
 ROWS_PER_PARTITION = 4
 PAIR = CHILDREN // ROWS_PER_PARTITION
@@ -352,17 +353,17 @@ def tile_childsumtreelstmcell_pb_kernel(
         quantise("uu", 0, 1)
         quantise_nodes(h_q, h_grouped, P * 0, P * 1)
         regroup(vcopy, "uu", 1, 0, HALF)
-        regroup(vcopy, "uu", 1, HALF, HALF + P)
-        regroup(scopy, "uu", 1, HALF + P, HIDDEN)
+        regroup(vcopy, "uu", 1, HALF, HALF + EXTRA)
+        regroup(scopy, "uu", 1, HALF + EXTRA, HIDDEN)
         acc["i", 0, 0] = products("wi", "ui", 0, 0)
         activate_tile(acc["i", 0, 0], GATE_I, ACT.Sigmoid, 0, 0, i_gate)
         acc["i", 1, 0] = products("wi", "ui", 1, 0)
         activate_tile(acc["i", 1, 0], GATE_I, ACT.Sigmoid, 1, 0, i_gate)
         quantise("uu", 1, 0)
         regroup(vcopy, "wo", 0, 0, HALF)
-        regroup(vcopy, "wo", 0, HALF, HALF + P)
+        regroup(vcopy, "wo", 0, HALF, HALF + EXTRA)
         quantise("uu", 1, 1)
-        regroup(scopy, "wo", 0, HALF + P, HALF + Q)
+        regroup(scopy, "wo", 0, HALF + EXTRA, HALF + Q)
         acc["u", 0, 0] = products("wu", "uu", 0, 0)
         activate_tile(acc["u", 0, 0], GATE_U, ACT.Tanh, 0, 0, u_gate)
         regroup(scopy, "wo", 0, HALF + Q, HIDDEN)
@@ -370,7 +371,7 @@ def tile_childsumtreelstmcell_pb_kernel(
         activate_tile(acc["u", 1, 0], GATE_U, ACT.Tanh, 1, 0, u_gate)
         quantise("wo", 0, 0)
         regroup(vcopy, "wo", 1, 0, HALF)
-        regroup(vcopy, "wo", 1, HALF, HALF + P)
+        regroup(vcopy, "wo", 1, HALF, HALF + EXTRA)
         multiply_gates(0, 0)
         quantise("wo", 1, 0)
         sums[2, 0] = sum_children(2, 0)
@@ -378,7 +379,7 @@ def tile_childsumtreelstmcell_pb_kernel(
         flips[0, 0] = flip_back(u_gate, 0, 0)
         multiply_gates(1, 0)
         flips[1, 0] = flip_back(u_gate, 1, 0)
-        regroup(scopy, "wo", 1, HALF + P, HALF + Q)
+        regroup(scopy, "wo", 1, HALF + EXTRA, HALF + Q)
         regroup(scopy, "wo", 1, HALF + Q, HIDDEN)
         interleave_sums(scopy, sums[2, 0], 2, 0)
         interleave_sums(scopy, sums[2, 1], 2, 1)
@@ -394,6 +395,7 @@ def tile_childsumtreelstmcell_pb_kernel(
         quantise_nodes(h_q, h_grouped, P * 1, P * 2)
         cell_state(flips[1, 0], 1, 0)
         regroup(scopy, "uo", 0, HALF * 0 + V, HALF * 1)
+        tanh_cell(1, 0)
         regroup(scopy, "uo", 0, HALF * 1 + V, HALF * 2)
         regroup(vcopy, "uo", 0, HALF * 0, HALF * 0 + V)
         acc["i", 0, 1] = products("wi", "ui", 0, 1)
@@ -406,7 +408,6 @@ def tile_childsumtreelstmcell_pb_kernel(
         acc["i", 1, 1] = products("wi", "ui", 1, 1)
         regroup(scopy, "uo", 1, HALF * 0 + V, HALF * 1)
         regroup(vcopy, "uo", 1, HALF * 0, HALF * 0 + V)
-        tanh_cell(1, 0)
         multiply_gates(0, 1)
         activate_tile(acc["u", 1, 1], GATE_U, ACT.Tanh, 1, 1, u_gate)
         activate_tile(acc["i", 1, 1], GATE_I, ACT.Sigmoid, 1, 1, i_gate)

@@ -102,11 +102,12 @@ def tile_childsumtreelstmcell_pb_kernel(
             half = first // HALF
             if (label, g, half) not in regrouped:
                 regrouped[label, g, half] = grouped_pool.tile([P, HALF, PACK], BF16, align_bytes=64, name="grouped")
+            run = 4 if copy is vcopy else 8
             copy(
                 out=regrouped[label, g, half][:, first - HALF * half : end - HALF * half, :].rearrange(
-                    "p (c i) t -> p c t i", i=8
+                    "p (c i) t -> p c t i", i=run
                 ),
-                in_=raws[label, g][:, :, first:end].rearrange("p t (c i) -> p c t i", i=8),
+                in_=raws[label, g][:, :, first:end].rearrange("p t (c i) -> p c t i", i=run),
             )
 
         def quantise(label, g, half, first=0, end=HALF):

from contextlib import ExitStack

import concourse.mybir as mybir
from concourse.masks import make_identity

F32 = mybir.dt.float32
BF16 = mybir.dt.bfloat16
U32 = mybir.dt.uint32
U8 = mybir.dt.uint8
FP8X4 = mybir.dt.float8_e4m3fn_x4
ACT = mybir.ActivationFunctionType
ALU = mybir.AluOpType

P = 128
PACK = 4
K_PASS = P * PACK
NODES = 256
NODE_TILES = NODES // P
CHILDREN = 8
FEATURES = 1024
PASSES = FEATURES // K_PASS
HIDDEN = 1024
COL_TILES = HIDDEN // P
BANK = 512
HALF = HIDDEN // 2
TILES_PER_HALF = HALF // P
EXTRA = 64

ROWS_PER_PARTITION = 4
PAIR = CHILDREN // ROWS_PER_PARTITION
NODES_PER_LOAD = P // PAIR

GATE_I, GATE_U, GATE_O = 0, 1, 2

FLOPS = 2 * NODES * FEATURES * HIDDEN * 6


def tile_childsumtreelstmcell_pb_kernel(
    tc, x, child_h, fc_sum, Wi, bWi, Ui, bUi, Wo, bWo, Uo, bUo, Wu, bWu, Uu, bUu, out
):
    nc = tc.nc
    with ExitStack() as ctx:
        ctx.enter_context(tc.manual_schedule())
        const = ctx.enter_context(tc.tile_pool(name="const", bufs=1))
        keep = ctx.enter_context(tc.tile_pool(name="keep", bufs=1))
        raw_pool = ctx.enter_context(tc.tile_pool(name="raw", bufs=6))
        grouped_pool = ctx.enter_context(tc.tile_pool(name="grouped", bufs=6))
        child_pool = ctx.enter_context(tc.tile_pool(name="child", bufs=4))
        psum = ctx.enter_context(tc.psum_pool(name="psum", bufs=8))

        ident = const.tile([P, P], F32)
        make_identity(nc, ident[:])
        pair_sum_f32 = const.tile([P, P // PAIR], F32)
        nc.vector.reduce_sum(
            out=pair_sum_f32[:], in_=ident[:].rearrange("q (i r) -> q i r", r=PAIR), axis=mybir.AxisListType.X
        )
        pair_sum = const.tile([P, P // PAIR], BF16)
        nc.vector.tensor_copy(out=pair_sum[:], in_=pair_sum_f32[:])

        zero_col = const.tile([P, 1], F32)
        nc.vector.memset(zero_col[:], 0.0)
        half_col = const.tile([P, 1], F32)
        nc.scalar.activation(out=half_col[:], in_=zero_col[:], func=ACT.Sigmoid)

        bias_rows = const.tile([P, P], BF16)
        nc.vector.memset(bias_rows[:], 0.0)
        bias = const.tile([P, P // PAIR], F32)

        bias_vectors = [(m, r, b) for m, pair in enumerate(((bWi, bUi), (bWu, bUu), (bWo, bUo))) for r, b in enumerate(pair)]

        def load_bias():
            m, r, b = bias_vectors.pop()
            first = PAIR * COL_TILES * m + r
            nc.sync.dma_start(
                out=bias_rows[first : PAIR * COL_TILES * (m + 1) : PAIR, :],
                in_=b.rearrange("(j p) -> j p", p=P),
            )

        def sum_biases():
            bias_ps = psum.tile([P, P // PAIR], F32, tag="bank")
            nc.tensor.matmul(out=bias_ps[:], lhsT=bias_rows[:], rhs=pair_sum[:], start=True, stop=True)
            nc.vector.tensor_copy(out=bias[:], in_=bias_ps[:])

        weights = {"wi": Wi, "ui": Ui, "wu": Wu, "uu": Uu, "wo": Wo, "uo": Uo}
        raws, words, scales, regrouped = {}, {}, {}, {}

        def load_weight(label, g, pieces=1):
            raw = raw_pool.tile([P, PACK, HIDDEN], BF16, name="raw")
            rows = weights[label][K_PASS * g : K_PASS * (g + 1), :].rearrange("(p t) n -> p t n", t=PACK)
            width = HIDDEN // pieces
            for c in range(pieces):
                cols = slice(width * c, width * (c + 1))
                nc.sync.dma_start(out=raw[:, :, cols], in_=rows[:, :, cols])
            raws[label, g] = raw
            words[label, g] = keep.tile([P, HIDDEN], U32, align_bytes=64, name="words_%s%d" % (label, g))
            scales[label, g] = keep.tile([P, HIDDEN], U8, align_bytes=64, name="scales_%s%d" % (label, g))

        def load_fc(a):
            nc.sync.dma_start(out=fc_sb[:, a, :], in_=fc_sum[P * a : P * (a + 1), :])

        def regroup(copy, label, g, first, end):
            half = first // HALF
            if (label, g, half) not in regrouped:
                regrouped[label, g, half] = grouped_pool.tile([P, HALF, PACK], BF16, align_bytes=64, name="grouped")
            run = 4 if copy is vcopy else 8
            copy(
                out=regrouped[label, g, half][:, first - HALF * half : end - HALF * half, :].rearrange(
                    "p (c i) t -> p c t i", i=run
                ),
                in_=raws[label, g][:, :, first:end].rearrange("p t (c i) -> p c t i", i=run),
            )

        def quantise(label, g, half, first=0, end=HALF):
            cols = slice(HALF * half + first, HALF * half + end)
            nc.vector.quantize_mx(
                out=words[label, g][:, cols].bitcast(FP8X4),
                scales=scales[label, g][:, cols],
                in_=regrouped[label, g, half][:, first:end, :].rearrange("p n t -> p (n t)"),
            )

        def load_child():
            child = child_pool.tile([P, ROWS_PER_PARTITION, FEATURES], BF16, name="child")
            nc.sync.dma_start(out=child[:], in_=child_rows[len(children)])
            children.append(child)

        def sum_children(l, g):
            by_word = children[l][:].rearrange("q s (g p t) -> q s g t p", g=PASSES, t=PACK)
            h_ps = psum.tile([P, PACK, NODES_PER_LOAD], F32, tag="bank", name="h_ps")
            for t in range(PACK):
                for s in range(ROWS_PER_PARTITION):
                    nc.tensor.matmul(
                        out=h_ps[:, t, :],
                        lhsT=by_word[:, s, g, t, :],
                        rhs=pair_sum[:],
                        start=(s == 0),
                        stop=(s == ROWS_PER_PARTITION - 1),
                    )
            return h_ps

        def interleave_sums(copy, h_ps, l, g):
            first = NODES_PER_LOAD * l
            copy(
                out=h_grouped[:, g, first : first + NODES_PER_LOAD, :],
                in_=h_ps[:].rearrange("p t n -> p n t"),
            )

        def quantise_nodes(operand, grouped, first, end, passes=range(PASSES)):
            node_words, node_scales = operand
            for g in passes:
                nc.vector.quantize_mx(
                    out=node_words[:, g, first:end].bitcast(FP8X4),
                    scales=node_scales[:, g, first:end],
                    in_=grouped[:, g, first:end, :].rearrange("p n t -> p (n t)"),
                )

        def mx_pass(acc, key, operand, first=False, last=False, tiles=range(TILES_PER_HALF)):
            label, g, half = key
            node_words, node_scales = operand
            for q in tiles:
                cols = slice(HALF * half + P * q, HALF * half + P * (q + 1))
                nc.tensor.matmul_mx(
                    out=acc[q][:],
                    lhsT=words[label, g][:, cols].bitcast(FP8X4),
                    lhsT_scale=scales[label, g][:, cols],
                    rhs=node_words[:, g, :].bitcast(FP8X4),
                    rhs_scale=node_scales[:, g, :],
                    start=first,
                    stop=last,
                )

        def open_gate(w, half, tiles=range(TILES_PER_HALF)):
            opened = {q: psum.tile([P, NODES], F32, tag="bank", name="acc") for q in tiles}
            for g in range(PASSES):
                mx_pass(opened, (w, g, half), x_q, first=(g == 0), tiles=tiles)
            return opened

        def activate(acc, m, func, half, result, tiles=range(TILES_PER_HALF)):
            for q in tiles:
                j = TILES_PER_HALF * half + q
                nc.scalar.activation(
                    out=result[:, j, :],
                    in_=acc[q][:],
                    func=func,
                    bias=bias[:, COL_TILES * m + j : COL_TILES * m + j + 1],
                )

        def products(w, u, half, a):
            acc = psum.tile([P, TILES_PER_HALF, P], F32, tag="bank", name="acc_tile")
            nodes = slice(P * a, P * (a + 1))
            passes = [(label, g, operand) for label, operand in ((w, x_q), (u, h_q)) for g in range(PASSES)]
            for q in range(TILES_PER_HALF):
                cols = slice(HALF * half + P * q, HALF * half + P * (q + 1))
                for n, (label, g, (node_words, node_scales)) in enumerate(passes):
                    nc.tensor.matmul_mx(
                        out=acc[:, q, :],
                        lhsT=words[label, g][:, cols].bitcast(FP8X4),
                        lhsT_scale=scales[label, g][:, cols],
                        rhs=node_words[:, g, nodes].bitcast(FP8X4),
                        rhs_scale=node_scales[:, g, nodes],
                        start=(n == 0),
                        stop=(n == len(passes) - 1),
                    )
            return acc

        def activate_tile(acc, m, func, half, a, result):
            for q in range(TILES_PER_HALF):
                j = TILES_PER_HALF * half + q
                nc.scalar.activation(
                    out=result[:, j, P * a : P * (a + 1)],
                    in_=acc[:, q, :],
                    func=func,
                    bias=bias[:, COL_TILES * m + j : COL_TILES * m + j + 1],
                )

        def flip_back(source, half, a, tiles=range(TILES_PER_HALF)):
            flipped = psum.tile([P, P * len(tiles)], F32, tag="bank", name="flipped")
            for n, q in enumerate(tiles):
                nc.tensor.transpose(
                    flipped[:, P * n : P * (n + 1)],
                    source[:, TILES_PER_HALF * half + q, P * a : P * (a + 1)],
                    ident[:],
                )
            return flipped

        def multiply_gates(half, a):
            tiles = slice(TILES_PER_HALF * half, TILES_PER_HALF * (half + 1))
            nodes = slice(P * a, P * (a + 1))
            nc.vector.tensor_tensor(
                out=u_gate[:, tiles, nodes], in0=i_gate[:, tiles, nodes], in1=u_gate[:, tiles, nodes], op=ALU.mult
            )

        def cell_state(iu_flipped, half, a):
            cols = slice(HALF * half, HALF * (half + 1))
            nc.vector.tensor_tensor(
                out=c_sb[:, a, cols], in0=iu_flipped[:], in1=fc_sb[:, a, cols], op=ALU.add
            )
            nc.sync.dma_start(out=out[1, P * a : P * (a + 1), cols], in_=c_sb[:, a, cols])

        def tanh_cell(half, a):
            cols = slice(HALF * half, HALF * (half + 1))
            nc.scalar.activation(out=tanh_c[:, a, cols], in_=c_sb[:, a, cols], func=ACT.Tanh)

        def hidden_state(o_flipped, half, a, tiles=range(TILES_PER_HALF)):
            cols = slice(HALF * half + P * tiles[0], HALF * half + P * (tiles[-1] + 1))
            nc.vector.tensor_tensor(
                out=tanh_c[:, a, cols], in0=o_flipped[:], in1=tanh_c[:, a, cols], op=ALU.mult
            )
            nc.sync.dma_start(out=out[0, P * a : P * (a + 1), cols], in_=tanh_c[:, a, cols])

        def interleave_x(copy, a):
            x_ps = psum.tile([P, PASSES, 2, P], F32, tag="bank")
            for g in range(PASSES):
                for u in range(2):
                    nc.tensor.transpose(
                        x_ps[:, g, u, :],
                        x_words[:, a, (K_PASS // 2) * g + u : (K_PASS // 2) * (g + 1) : 2],
                        ident[:],
                    )
            copy(
                out=x_grouped[:, :, P * a : P * (a + 1), :].bitcast(F32), in_=x_ps[:].rearrange("p g u n -> p g n u")
            )

        child_rows = child_h.rearrange("n c k -> (n c) k").rearrange(
            "(l q s) k -> l q s k", q=P, s=ROWS_PER_PARTITION
        )
        children = []
        node_operands = []
        for label in ("x", "h"):
            node_words = keep.tile([P, PASSES, NODES], U32, align_bytes=64, name="words_" + label)
            node_scales = keep.tile([P, PASSES, NODES], U8, align_bytes=64, name="scales_" + label)
            node_operands.append((node_words, node_scales))
        x_q, h_q = node_operands
        x_sb = keep.tile([P, NODE_TILES, FEATURES], BF16)
        x_words = x_sb[:].bitcast(F32)
        x_grouped = keep.tile([P, PASSES, NODES, PACK], BF16, align_bytes=64)
        h_grouped = keep.tile([P, PASSES, NODES, PACK], BF16, align_bytes=64)
        fc_sb = keep.tile([P, NODE_TILES, HIDDEN], BF16)
        i_gate = keep.tile([P, COL_TILES, NODES], F32)
        u_gate = keep.tile([P, COL_TILES, NODES], F32)
        o_gate = keep.tile([P, COL_TILES, NODES], F32)
        c_sb = keep.tile([P, NODE_TILES, HIDDEN], F32)
        tanh_c = keep.tile([P, NODE_TILES, HIDDEN], F32)
        vcopy, scopy = nc.vector.tensor_copy, nc.scalar.copy

        Q = HALF // 2
        V = 384
        acc, sums, flips = {}, {}, {}
        load_weight("wi", 0, pieces=4)
        load_weight("wi", 1)
        load_bias()
        nc.sync.dma_start(out=x_sb[:], in_=x.rearrange("(a p) k -> p a k", p=P))
        load_bias()
        load_weight("ui", 0)
        load_bias()
        load_weight("ui", 1)
        load_bias()
        load_weight("wu", 0)
        load_bias()
        load_weight("wu", 1)
        load_bias()
        regroup(vcopy, "wi", 0, HALF * 0, HALF * 0 + Q)
        regroup(scopy, "wi", 0, HALF * 0 + Q, HALF * 1)
        regroup(vcopy, "wi", 0, HALF * 1, HALF * 1 + Q)
        regroup(scopy, "wi", 0, HALF * 1 + Q, HALF * 2)
        load_weight("uu", 0)
        load_child()
        load_child()
        quantise("wi", 0, 0)
        regroup(vcopy, "wi", 1, 0, HALF)
        regroup(scopy, "wi", 1, HALF, HIDDEN)
        load_weight("uu", 1)
        quantise("wi", 0, 1)
        quantise("wi", 1, 0)
        interleave_x(scopy, 0)
        interleave_x(scopy, 1)
        regroup(vcopy, "ui", 0, 0, HALF)
        regroup(scopy, "ui", 0, HALF, HIDDEN)
        load_weight("wo", 0)
        quantise("wi", 1, 1)
        quantise("ui", 0, 0)
        quantise_nodes(x_q, x_grouped, 0, NODES)
        regroup(vcopy, "ui", 1, 0, HALF)
        regroup(scopy, "ui", 1, HALF, HIDDEN)
        load_weight("wo", 1)
        load_child()
        load_child()
        load_fc(0)
        quantise("ui", 0, 1)
        quantise("ui", 1, 0)
        regroup(vcopy, "wu", 0, 0, HALF)
        regroup(scopy, "wu", 0, HALF, HIDDEN)
        load_weight("uo", 0)
        quantise("ui", 1, 1)
        quantise("wu", 0, 0)
        sum_biases()
        regroup(vcopy, "wu", 1, 0, HALF)
        regroup(scopy, "wu", 1, HALF, HIDDEN)
        load_weight("uo", 1)
        load_fc(1)
        quantise("wu", 0, 1)
        quantise("wu", 1, 0)
        regroup(vcopy, "uu", 0, 0, HALF)
        regroup(scopy, "uu", 0, HALF, HIDDEN)
        quantise("wu", 1, 1)
        quantise("uu", 0, 0)
        sums[0, 0] = sum_children(0, 0)
        sums[0, 1] = sum_children(0, 1)
        interleave_sums(scopy, sums[0, 0], 0, 0)
        interleave_sums(scopy, sums[0, 1], 0, 1)
        sums[1, 0] = sum_children(1, 0)
        sums[1, 1] = sum_children(1, 1)
        interleave_sums(scopy, sums[1, 0], 1, 0)
        interleave_sums(scopy, sums[1, 1], 1, 1)
        quantise("uu", 0, 1)
        quantise_nodes(h_q, h_grouped, P * 0, P * 1)
        regroup(vcopy, "uu", 1, 0, HALF)
        regroup(vcopy, "uu", 1, HALF, HALF + EXTRA)
        regroup(scopy, "uu", 1, HALF + EXTRA, HIDDEN)
        acc["i", 0, 0] = products("wi", "ui", 0, 0)
        activate_tile(acc["i", 0, 0], GATE_I, ACT.Sigmoid, 0, 0, i_gate)
        acc["i", 1, 0] = products("wi", "ui", 1, 0)
        activate_tile(acc["i", 1, 0], GATE_I, ACT.Sigmoid, 1, 0, i_gate)
        quantise("uu", 1, 0)
        regroup(vcopy, "wo", 0, 0, HALF)
        regroup(vcopy, "wo", 0, HALF, HALF + EXTRA)
        quantise("uu", 1, 1)
        regroup(scopy, "wo", 0, HALF + EXTRA, HALF + Q)
        acc["u", 0, 0] = products("wu", "uu", 0, 0)
        activate_tile(acc["u", 0, 0], GATE_U, ACT.Tanh, 0, 0, u_gate)
        regroup(scopy, "wo", 0, HALF + Q, HIDDEN)
        acc["u", 1, 0] = products("wu", "uu", 1, 0)
        activate_tile(acc["u", 1, 0], GATE_U, ACT.Tanh, 1, 0, u_gate)
        quantise("wo", 0, 0)
        regroup(vcopy, "wo", 1, 0, HALF)
        regroup(vcopy, "wo", 1, HALF, HALF + EXTRA)
        multiply_gates(0, 0)
        quantise("wo", 1, 0)
        sums[2, 0] = sum_children(2, 0)
        sums[2, 1] = sum_children(2, 1)
        flips[0, 0] = flip_back(u_gate, 0, 0)
        multiply_gates(1, 0)
        flips[1, 0] = flip_back(u_gate, 1, 0)
        regroup(scopy, "wo", 1, HALF + EXTRA, HALF + Q)
        regroup(scopy, "wo", 1, HALF + Q, HIDDEN)
        interleave_sums(scopy, sums[2, 0], 2, 0)
        interleave_sums(scopy, sums[2, 1], 2, 1)
        sums[3, 0] = sum_children(3, 0)
        sums[3, 1] = sum_children(3, 1)
        acc["o", 0] = open_gate("wo", 0)
        quantise("wo", 0, 1)
        interleave_sums(scopy, sums[3, 0], 3, 0)
        interleave_sums(scopy, sums[3, 1], 3, 1)
        quantise("wo", 1, 1)
        cell_state(flips[0, 0], 0, 0)
        tanh_cell(0, 0)
        quantise_nodes(h_q, h_grouped, P * 1, P * 2)
        cell_state(flips[1, 0], 1, 0)
        regroup(scopy, "uo", 0, HALF * 0 + V, HALF * 1)
        tanh_cell(1, 0)
        regroup(scopy, "uo", 0, HALF * 1 + V, HALF * 2)
        regroup(vcopy, "uo", 0, HALF * 0, HALF * 0 + V)
        acc["i", 0, 1] = products("wi", "ui", 0, 1)
        activate_tile(acc["i", 0, 1], GATE_I, ACT.Sigmoid, 0, 1, i_gate)
        acc["u", 0, 1] = products("wu", "uu", 0, 1)
        regroup(vcopy, "uo", 0, HALF * 1, HALF * 1 + V)
        activate_tile(acc["u", 0, 1], GATE_U, ACT.Tanh, 0, 1, u_gate)
        quantise("uo", 0, 0)
        acc["u", 1, 1] = products("wu", "uu", 1, 1)
        acc["i", 1, 1] = products("wi", "ui", 1, 1)
        regroup(scopy, "uo", 1, HALF * 0 + V, HALF * 1)
        regroup(vcopy, "uo", 1, HALF * 0, HALF * 0 + V)
        multiply_gates(0, 1)
        activate_tile(acc["u", 1, 1], GATE_U, ACT.Tanh, 1, 1, u_gate)
        activate_tile(acc["i", 1, 1], GATE_I, ACT.Sigmoid, 1, 1, i_gate)
        quantise("uo", 1, 0)
        mx_pass(acc["o", 0], ("uo", 0, 0), h_q)
        mx_pass(acc["o", 0], ("uo", 1, 0), h_q, last=True)
        acc["o", 1] = open_gate("wo", 1, range(0, 2))
        quantise("uo", 0, 1)
        mx_pass(acc["o", 1], ("uo", 0, 1), h_q, tiles=range(0, 2))
        flips[0, 1] = flip_back(u_gate, 0, 1)
        activate(acc["o", 0], GATE_O, ACT.Sigmoid, 0, o_gate)
        regroup(scopy, "uo", 1, HALF * 1 + V, HALF * 2)
        regroup(vcopy, "uo", 1, HALF * 1, HALF * 1 + V)
        multiply_gates(1, 1)
        quantise("uo", 1, 1, P * 0, P * 2)
        flips["o", 0, 0] = flip_back(o_gate, 0, 0)
        flips[1, 1] = flip_back(u_gate, 1, 1)
        cell_state(flips[0, 1], 0, 1)
        tanh_cell(0, 1)
        flips["o", 0, 1] = flip_back(o_gate, 0, 1)
        mx_pass(acc["o", 1], ("uo", 1, 1), h_q, last=True, tiles=range(0, 2))
        activate(acc["o", 1], GATE_O, ACT.Sigmoid, 1, o_gate, range(0, 2))
        acc["o", 1].update(open_gate("wo", 1, range(2, 4)))
        mx_pass(acc["o", 1], ("uo", 0, 1), h_q, tiles=range(2, 4))
        quantise("uo", 1, 1, P * 2, P * 4)
        cell_state(flips[1, 1], 1, 1)
        mx_pass(acc["o", 1], ("uo", 1, 1), h_q, last=True, tiles=range(2, 4))
        tanh_cell(1, 1)
        hidden_state(flips["o", 0, 0], 0, 0)
        hidden_state(flips["o", 0, 1], 0, 1)
        flips["o", 1, 0] = flip_back(o_gate, 1, 0, range(0, 2))
        flips["o", 1, 1] = flip_back(o_gate, 1, 1, range(0, 2))
        activate(acc["o", 1], GATE_O, ACT.Sigmoid, 1, o_gate, range(2, 4))
        hidden_state(flips["o", 1, 0], 1, 0, range(0, 2))
        hidden_state(flips["o", 1, 1], 1, 1, range(0, 2))
        flips["o", 1, 0] = flip_back(o_gate, 1, 0, range(2, 4))
        hidden_state(flips["o", 1, 0], 1, 0, range(2, 4))
        flips["o", 1, 1] = flip_back(o_gate, 1, 1, range(2, 4))
        hidden_state(flips["o", 1, 1], 1, 1, range(2, 4))
